import numpy as np
import ml_dtypes


def mxq(x, axis, fmt="e4m3"):
    dtype, down = {"e4m3": (ml_dtypes.float8_e4m3fn, 7), "e5m2": (ml_dtypes.float8_e5m2, 14)}[fmt]
    v = np.moveaxis(np.asarray(x, np.float32).astype(ml_dtypes.bfloat16).astype(np.float64), axis, -1)
    blocks = v.reshape(v.shape[:-1] + (-1, 32))
    amax = np.abs(blocks).max(-1, keepdims=True)
    byte = np.maximum(np.where(amax > 0, np.frexp(amax)[1] - 1 + 127, 0) - down, 1)
    scale = np.exp2(byte - 127.0)
    codes = (blocks / scale).astype(np.float32).astype(dtype).astype(np.float64)
    return np.moveaxis((codes * scale).reshape(v.shape), -1, axis)


WIDE = False


def mx_kscale(k):
    if not WIDE:
        return np.ones(k)
    levels = np.array([10, -10, 5, -5, 0])
    a = np.random.permutation(np.resize(levels, k // 512 * 4)).reshape(k // 512, 4)
    idx = np.arange(k)
    return np.exp2(a[idx // 512, idx % 128 // 32])


BF16 = ml_dtypes.bfloat16


def bf(x):
    return np.asarray(x, np.float32).astype(BF16)


def f64(x):
    return np.asarray(x).astype(np.float64)


B, S, H, D, QB, DEPTH = 12, 512, 4, 128, 512, 12
HP = H // 2
LAMBDA_INIT = 0.8 - 0.6 * np.exp(-0.3 * DEPTH)
NEG_INF = -1e30
EPS = 1e-5


def split_heads(x):
    x = x.reshape(x.shape[0], x.shape[1], x.shape[2] // 2, 2, x.shape[3])
    return x[..., 0, :], x[..., 1, :]


def causal_attn(q, k, vq):
    rows = []
    for r0 in range(0, S, QB):
        r1 = r0 + QB
        s = (q[:, :, r0:r1] @ k[:, :, :r1].transpose(0, 1, 3, 2)) * (1.0 / np.sqrt(D))
        causal = np.arange(r0, r1)[:, None] >= np.arange(r1)[None, :]
        s = np.where(causal, s, NEG_INF)
        e = np.exp(s - s.max(-1, keepdims=True))
        rows.append((mxq(e, 3, "e4m3") @ vq[:, :, :r1]) / e.sum(-1, keepdims=True))
    return np.concatenate(rows, axis=2)


def setup_inputs():
    ls = 0.5 / D ** 0.25
    t = mx_kscale(S)
    qc = 0.25 * np.sqrt(D)
    q = np.random.standard_normal((B, S, H, D))
    k = np.random.standard_normal((B, S, H, D))
    v = np.random.standard_normal((B, S, H, D)) * 0.125
    q[..., 0] = qc
    k[..., 0] += (np.log(t) * np.sqrt(D) / qc)[None, :, None]
    v *= (t.mean() / t)[None, :, None, None]
    return {
        "q": bf(q),
        "k": bf(k),
        "v": bf(v),
        "lambda_q1": bf(np.random.standard_normal(D) * ls),
        "lambda_k1": bf(np.random.standard_normal(D) * ls),
        "lambda_q2": bf(np.random.standard_normal(D) * ls),
        "lambda_k2": bf(np.random.standard_normal(D) * ls),
        "subln_weight": bf(1.0 + 0.1 * np.random.standard_normal(2 * D)),
    }


def reference(q, k, v, lambda_q1, lambda_k1, lambda_q2, lambda_k2, subln_weight):
    q1, q2 = split_heads(f64(q))
    k1, k2 = split_heads(f64(k))
    v1, v2 = split_heads(f64(v))
    v12 = np.concatenate([v1, v2], axis=-1)
    vq = mxq(v12.transpose(0, 2, 1, 3), 2, "e4m3")
    attn1 = causal_attn(q1.transpose(0, 2, 1, 3), k1.transpose(0, 2, 1, 3), vq)
    attn2 = causal_attn(q2.transpose(0, 2, 1, 3), k2.transpose(0, 2, 1, 3), vq)
    lam1 = np.exp(np.sum(f64(lambda_q1) * f64(lambda_k1)))
    lam2 = np.exp(np.sum(f64(lambda_q2) * f64(lambda_k2)))
    lam = lam1 - lam2 + LAMBDA_INIT
    x = attn1 - lam * attn2
    var = np.mean(x * x, axis=-1, keepdims=True)
    xn = f64(subln_weight) * (x / np.sqrt(var + EPS))
    y = xn * (1.0 - LAMBDA_INIT)
    return y.transpose(0, 2, 1, 3).reshape(B, S, H, D)

@@ -1,0 +1,418 @@
+import math
+from contextlib import ExitStack
+
+import concourse.mybir as mybir
+from concourse.masks import make_identity
+
+BF16 = mybir.dt.bfloat16
+F32 = mybir.dt.float32
+U32 = mybir.dt.uint32
+U8 = mybir.dt.uint8
+FP8X4 = mybir.dt.float8_e4m3fn_x4
+ALU = mybir.AluOpType
+ACT = mybir.ActivationFunctionType
+AXIS_X = mybir.AxisListType.X
+
+B, S, H, D = 12, 512, 4, 128
+P = 128
+PAIRS = H // 2
+QT = S // P
+PACK = 4
+DEPTH = 12
+LAMBDA_INIT = 0.8 - 0.6 * math.exp(-0.3 * DEPTH)
+NEG_INF = -1e30
+EPS = 1e-5
+SCALE = 1.0 / math.sqrt(D)
+E_SLOTS = 2
+N_HALF = B * PAIRS * 2
+
+FLOPS = 2 * B * H * S * S * D + 2 * B * H * S * S * 2 * D
+
+
+def tile_refphi4flashdiffattention_pa_t_kernel(
+    tc, q, k, v, lambda_q1, lambda_k1, lambda_q2, lambda_k2, subln_weight, out
+):
+    nc = tc.nc
+    with ExitStack() as stack:
+        const = stack.enter_context(tc.tile_pool(name="const", bufs=1))
+        loads = stack.enter_context(tc.tile_pool(name="loads", bufs=3))
+        work = stack.enter_context(tc.tile_pool(name="work", bufs=4))
+        stats = stack.enter_context(tc.tile_pool(name="stats", bufs=6))
+        psum_tp = stack.enter_context(tc.psum_pool(name="psum_tp", bufs=1))
+        psum_s = stack.enter_context(tc.psum_pool(name="psum_s", bufs=3))
+        psum_et = stack.enter_context(tc.psum_pool(name="psum_et", bufs=2))
+        psum_o = stack.enter_context(tc.psum_pool(name="psum_o", bufs=2))
+        stack.enter_context(tc.manual_schedule())
+
+        ident_bf = const.tile([P, P], BF16, name="ident_bf")
+        make_identity(nc, ident_bf[:])
+        ident_f32 = const.tile([P, P], F32, name="ident_f32")
+        make_identity(nc, ident_f32[:])
+        mask_f32 = const.tile([P, P], F32, name="mask_f32")
+        nc.gpsimd.memset(mask_f32[:], 0.0)
+        nc.gpsimd.affine_select(
+            out=mask_f32[:],
+            in_=mask_f32[:],
+            pattern=[[-1, P]],
+            compare_op=ALU.is_ge,
+            fill=NEG_INF,
+            base=0,
+            channel_multiplier=1,
+        )
+        mask_bf = const.tile([P, P], BF16, name="mask_bf")
+        nc.vector.tensor_copy(out=mask_bf[:], in_=mask_f32[:])
+        neg_half = const.tile([P, 2], F32, name="neg_half")
+        nc.vector.memset(neg_half[:], -0.5)
+
+        e_tiles = {}
+        for slot in range(E_SLOTS):
+            for hh in range(2):
+                for i in range(QT):
+                    e_t = const.tile([P, S], BF16, name="e_%d_%d_%d" % (slot, hh, i))
+                    if i < QT - 1:
+                        nc.vector.memset(e_t[:, (i + 1) * P :], 0.0)
+                    e_tiles[(slot, hh, i)] = e_t
+
+        lam_in = const.tile([P, 4, D], BF16, name="lam_in")
+        w_in = const.tile([P, 2 * D], BF16, name="w_in")
+        lam = const.tile([P, 1], F32, name="lam")
+        gain = const.tile([P, 2 * D], F32, name="gain")
+
+        inputs = {}
+        v_mx = {}
+        qk_banks = {}
+        qk_t = {}
+        score_banks = {}
+        scores = {}
+        rowsums = {}
+        word_banks = {}
+        grouped = {}
+        e_mx = {}
+        factors = {}
+        out_banks = {}
+        seconds = {}
+        xs = {}
+        mean_sqs = {}
+
+        def load_batch(b):
+            if b >= B:
+                return
+            q_sb = loads.tile([P, QT, H * D], BF16, name="q_sb")
+            nc.sync.dma_start(out=q_sb[:], in_=q[b].rearrange("(t p) h d -> p t (h d)", p=P))
+            k_sb = loads.tile([P, QT, H * D], BF16, name="k_sb")
+            nc.sync.dma_start(out=k_sb[:], in_=k[b].rearrange("(t p) h d -> p t (h d)", p=P))
+            v_sb = loads.tile([P, PACK, H * D], BF16, name="v_sb")
+            nc.sync.dma_start(
+                out=v_sb[:].rearrange("p (u e) f -> p u (e f)", u=2),
+                in_=v[b].rearrange("(u p e) h d -> p u (e h d)", u=2, e=2),
+            )
+            inputs[b] = (q_sb, k_sb, v_sb)
+
+        def load_small():
+            for c, vec in enumerate((lambda_q1, lambda_q2, lambda_k1, lambda_k2)):
+                nc.sync.dma_start(out=lam_in[:, c, :], in_=vec.partition_broadcast(P))
+            nc.sync.dma_start(out=w_in[:], in_=subln_weight.partition_broadcast(P))
+
+        def lam_and_gain():
+            prod = const.tile([P, 2, D], F32, name="prod")
+            nc.vector.tensor_tensor(
+                out=prod[:], in0=lam_in[:, 0:2, :], in1=lam_in[:, 2:4, :], op=ALU.mult
+            )
+            dots = const.tile([P, 2], F32, name="dots")
+            nc.vector.tensor_reduce(out=dots[:], in_=prod[:], axis=AXIS_X, op=ALU.add)
+            exps = const.tile([P, 2], F32, name="exps")
+            nc.scalar.activation(out=exps[:], in_=dots[:], func=ACT.Exp)
+            nc.vector.tensor_scalar(
+                out=lam[:],
+                in0=exps[:, 0:1],
+                scalar1=exps[:, 1:2],
+                scalar2=LAMBDA_INIT,
+                op0=ALU.subtract,
+                op1=ALU.add,
+            )
+            nc.vector.tensor_scalar(
+                out=gain[:], in0=w_in[:], scalar1=1.0 - LAMBDA_INIT, scalar2=None, op0=ALU.mult
+            )
+
+        def regroup_v(b):
+            if b >= B:
+                return
+            v_sb = inputs[b][2]
+            v_grouped = work.tile([P, H * D, PACK], BF16, name="v_grouped", bufs=2, align_bytes=64)
+            nc.vector.tensor_copy(
+                out=v_grouped[:].rearrange("p (c i) t -> p c t i", i=4),
+                in_=v_sb[:].rearrange("p t (c i) -> p c t i", i=4),
+            )
+            grouped[("v", b)] = v_grouped
+
+        def quantise_v(b):
+            if b >= B:
+                return
+            v_codes = work.tile([P, H * D], U32, name="v_codes", bufs=3, align_bytes=64)
+            v_scales = work.tile([P, H * D], U8, name="v_scales", bufs=3, align_bytes=64)
+            nc.vector.quantize_mx(
+                out=v_codes[:].bitcast(FP8X4),
+                scales=v_scales[:],
+                in_=grouped[("v", b)][:].rearrange("p f t -> p (f t)"),
+            )
+            v_mx[b] = (v_codes, v_scales)
+
+        def transpose_qk(unit, hh):
+            if unit >= B * PAIRS:
+                return
+            q_sb, k_sb = inputs[unit // PAIRS][0:2]
+            h = 2 * (unit % PAIRS) + hh
+            head_cols = slice(h * D, (h + 1) * D)
+            tp = psum_tp.tile([P, 2 * QT, P], BF16, name="tp")
+            for t in range(QT):
+                nc.tensor.transpose(tp[:, t, :], q_sb[:, t, head_cols], ident_bf[:])
+            for t in range(QT):
+                nc.tensor.transpose(tp[:, QT + t, :], k_sb[:, t, head_cols], ident_bf[:])
+            qk_banks[(unit, hh)] = tp
+
+        def copy_qk(unit, hh):
+            if unit >= B * PAIRS:
+                return
+            qk = work.tile([P, 2 * S], BF16, name="qk", bufs=6)
+            nc.scalar.copy(out=qk[:], in_=qk_banks[(unit, hh)][:].rearrange("p t c -> p (t c)"))
+            qk_t[(unit, hh)] = qk
+
+        def score_matmuls(j, tau):
+            if not 0 <= j < N_HALF:
+                return
+            hh, i = tau // 2, 2 * (j % 2) + tau % 2
+            q_t = qk_t[(j // 2, hh)][:, 0:S]
+            k_t = qk_t[(j // 2, hh)][:, S : 2 * S]
+            own = slice(i * P, (i + 1) * P)
+            s_ps = psum_s.tile([P, S], F32, name="s_ps")
+            nc.tensor.matmul(s_ps[:, own], lhsT=ident_bf[:], rhs=mask_bf[:], start=True, stop=False)
+            nc.tensor.matmul(s_ps[:, own], lhsT=q_t[:, own], rhs=k_t[:, own], start=False, stop=True)
+            if i > 0:
+                nc.tensor.matmul(
+                    s_ps[:, 0 : i * P], lhsT=q_t[:, own], rhs=k_t[:, 0 : i * P], start=True, stop=True
+                )
+            score_banks[(j, tau)] = s_ps
+
+        def row_maximum(j, tau):
+            if not 0 <= j < N_HALF:
+                return
+            n = (2 * (j % 2) + tau % 2 + 1) * P
+            s_sb = work.tile([P, S], F32, name="s_sb")
+            shift = stats.tile([P, 1], F32, name="shift")
+            nc.vector.tensor_scalar(
+                out=s_sb[:, 0:n],
+                in0=score_banks[(j, tau)][:, 0:n],
+                scalar1=-SCALE,
+                scalar2=None,
+                op0=ALU.mult,
+                op1=ALU.min,
+                accum_out=shift[:],
+            )
+            scores[(j, tau)] = (s_sb, shift)
+
+        def exponentials(j, tau):
+            if not 0 <= j < N_HALF:
+                return
+            hh, i = tau // 2, 2 * (j % 2) + tau % 2
+            n = (i + 1) * P
+            if tau == 0:
+                rowsums[j] = stats.tile([P, 4], F32, name="rowsum")
+            s_sb, shift = scores[(j, tau)]
+            nc.scalar.activation(
+                out=e_tiles[((j // 2) % E_SLOTS, hh, i)][:, 0:n],
+                in_=s_sb[:, 0:n],
+                func=ACT.Exp,
+                bias=shift[:],
+                scale=-1.0,
+                accum_out=rowsums[j][:, tau : tau + 1],
+            )
+
+        def transpose_e(j, hh):
+            if not 0 <= j < N_HALF:
+                return
+            et_ps = psum_et.tile([P, 2, 2, P], F32, name="et_ps")
+            for ii in range(2):
+                e_words = e_tiles[((j // 2) % E_SLOTS, hh, 2 * (j % 2) + ii)][:].bitcast(F32)
+                for u in range(2):
+                    nc.tensor.transpose(
+                        et_ps[:, ii, u, :], e_words[:, u * P : (u + 1) * P], ident_f32[:]
+                    )
+            word_banks[(j, hh)] = et_ps
+
+        def copy_e_words(j, hh):
+            if not 0 <= j < N_HALF:
+                return
+            e_grouped = work.tile([P, 2 * P * PACK], BF16, name="e_grouped", align_bytes=64)
+            dst = e_grouped[:].bitcast(F32).rearrange("p (i q u) -> p i q u", i=2, u=2)
+            src = word_banks[(j, hh)][:].rearrange("p i u q -> p i q u")
+            if hh == 0:
+                nc.vector.tensor_copy(out=dst, in_=src)
+            else:
+                nc.scalar.copy(out=dst, in_=src)
+            grouped[(j, hh)] = e_grouped
+
+        def quantise_e(j, hh):
+            if not 0 <= j < N_HALF:
+                return
+            codes = work.tile([P, 2 * P], U32, name="codes", bufs=6, align_bytes=64)
+            scales = work.tile([P, 2 * P], U8, name="scales", bufs=6, align_bytes=64)
+            nc.vector.quantize_mx(
+                out=codes[:].bitcast(FP8X4), scales=scales[:], in_=grouped[(j, hh)][:]
+            )
+            e_mx[(j, hh)] = (codes, scales)
+
+        def mx_passes(j):
+            if not 0 <= j < N_HALF:
+                return
+            v_codes, v_scales = v_mx[j // 4]
+            pair_cols = slice(((j // 2) % PAIRS) * 2 * D, ((j // 2) % PAIRS + 1) * 2 * D)
+            for ii in range(2):
+                q_cols = slice(ii * P, (ii + 1) * P)
+                o_ps = psum_o.tile([P, 2, 2 * D], F32, name="o_ps")
+                for hh in range(2):
+                    codes, scales = e_mx[(j, hh)]
+                    nc.tensor.matmul_mx(
+                        out=o_ps[:, hh, :],
+                        lhsT=codes[:, q_cols].bitcast(FP8X4),
+                        lhsT_scale=scales[:, q_cols],
+                        rhs=v_codes[:, pair_cols].bitcast(FP8X4),
+                        rhs_scale=v_scales[:, pair_cols],
+                        start=True,
+                        stop=True,
+                    )
+                out_banks[(j, ii)] = o_ps
+
+        def normalisers(j):
+            if not 0 <= j < N_HALF:
+                return
+            inv = stats.tile([P, 4], F32, name="inv")
+            nc.vector.reciprocal(out=inv[:], in_=rowsums[j][:])
+            lam_inv = stats.tile([P, 2], F32, name="lam_inv")
+            nc.vector.tensor_scalar(
+                out=lam_inv[:], in0=inv[:, 2:4], scalar1=lam[:], scalar2=None, op0=ALU.mult
+            )
+            factors[j] = (inv, lam_inv)
+
+        def scale_second(j, ii):
+            if not 0 <= j < N_HALF:
+                return
+            second = work.tile([P, 2 * D], F32, name="second")
+            nc.scalar.activation(
+                out=second[:],
+                in_=out_banks[(j, ii)][:, 1, :],
+                func=ACT.Copy,
+                scale=factors[j][1][:, ii : ii + 1],
+            )
+            seconds[(j, ii)] = second
+
+        def difference(j, ii):
+            if not 0 <= j < N_HALF:
+                return
+            if ii == 0:
+                xs[j] = work.tile([P, 2, 2 * D], F32, name="x")
+            nc.vector.scalar_tensor_tensor(
+                out=xs[j][:, ii, :],
+                in0=out_banks[(j, ii)][:, 0, :],
+                scalar=factors[j][0][:, ii : ii + 1],
+                in1=seconds[(j, ii)][:],
+                op0=ALU.mult,
+                op1=ALU.subtract,
+            )
+
+        def sum_squares(j, ii):
+            if not 0 <= j < N_HALF:
+                return
+            if ii == 0:
+                mean_sqs[j] = stats.tile([P, 2], F32, name="mean_sq")
+            squares = work.tile([P, 2 * D], F32, name="squares")
+            nc.scalar.activation(
+                out=squares[:],
+                in_=xs[j][:, ii, :],
+                func=ACT.Square,
+                scale=1.0 / math.sqrt(2 * D),
+                accum_out=mean_sqs[j][:, ii : ii + 1],
+            )
+
+        def finish(j):
+            if not 0 <= j < N_HALF:
+                return
+            b, pr, g = j // 4, (j // 2) % PAIRS, j % 2
+            xg = work.tile([P, 2, 2 * D], F32, name="xg")
+            nc.gpsimd.tensor_tensor(
+                out=xg[:],
+                in0=xs[j][:],
+                in1=gain[:].unsqueeze(1).to_broadcast([P, 2, 2 * D]),
+                op=ALU.mult,
+            )
+            var_eps = stats.tile([P, 2], F32, name="var_eps")
+            nc.gpsimd.tensor_scalar(
+                out=var_eps[:], in0=mean_sqs[j][:], scalar1=1.0, scalar2=EPS, op0=ALU.mult, op1=ALU.add
+            )
+            rstd = stats.tile([P, 2], F32, name="rstd")
+            nc.gpsimd.tensor_tensor(out=rstd[:], in0=var_eps[:], in1=neg_half[:], op=ALU.pow)
+            y = work.tile([P, 2, 2 * D], F32, name="y")
+            for ii in range(2):
+                nc.gpsimd.tensor_scalar(
+                    out=y[:, ii, :],
+                    in0=xg[:, ii, :],
+                    scalar1=rstd[:, ii : ii + 1],
+                    scalar2=0.0,
+                    op0=ALU.mult,
+                    op1=ALU.add,
+                )
+            nc.sync.dma_start(
+                out=out[b, g * 2 * P : (g + 1) * 2 * P, 2 * pr : 2 * pr + 2, :].rearrange(
+                    "(i p) h d -> p i (h d)", p=P
+                ),
+                in_=y[:],
+            )
+
+        load_batch(0)
+        load_small()
+        load_batch(1)
+        for j in range(-2, N_HALF + 3):
+            starts_unit = (j + 1) % 2 == 0
+            next_unit = (j + 1) // 2
+            if j >= 0 and j % 4 == 0:
+                load_batch(j // 4 + 2)
+            mx_passes(j - 2)
+            score_matmuls(j, 1)
+            sum_squares(j - 3, 1)
+            exponentials(j - 1, 3)
+            row_maximum(j, 0)
+            exponentials(j, 0)
+            normalisers(j - 2)
+            copy_e_words(j - 1, 0)
+            finish(j - 3)
+            scale_second(j - 2, 0)
+            score_matmuls(j, 2)
+            transpose_e(j - 1, 1)
+            if starts_unit:
+                transpose_qk(next_unit, 0)
+            scale_second(j - 2, 1)
+            row_maximum(j, 1)
+            if j == 0:
+                lam_and_gain()
+            if (j + 2) % 4 == 0:
+                regroup_v((j + 2) // 4)
+            if (j + 1) % 4 == 0:
+                quantise_v((j + 1) // 4)
+            score_matmuls(j, 3)
+            copy_e_words(j - 1, 1)
+            if starts_unit:
+                copy_qk(next_unit, 0)
+            row_maximum(j, 2)
+            exponentials(j, 1)
+            exponentials(j, 2)
+            quantise_e(j - 1, 0)
+            score_matmuls(j + 1, 0)
+            difference(j - 2, 0)
+            difference(j - 2, 1)
+            if starts_unit:
+                transpose_qk(next_unit, 1)
+            transpose_e(j, 0)
+            sum_squares(j - 2, 0)
+            row_maximum(j, 3)
+            if starts_unit:
+                copy_qk(next_unit, 1)
+            quantise_e(j - 1, 1)

@@ -39,7 +39,8 @@ def tile_refphi4flashdiffattention_pa_t_kernel(
         work = stack.enter_context(tc.tile_pool(name="work", bufs=4))
         stats = stack.enter_context(tc.tile_pool(name="stats", bufs=6))
         psum_tp = stack.enter_context(tc.psum_pool(name="psum_tp", bufs=1))
-        psum_s = stack.enter_context(tc.psum_pool(name="psum_s", bufs=3))
+        psum_s = stack.enter_context(tc.psum_pool(name="psum_s", bufs=2))
+        psum_x = stack.enter_context(tc.psum_pool(name="psum_x", bufs=1))
         psum_et = stack.enter_context(tc.psum_pool(name="psum_et", bufs=2))
         psum_o = stack.enter_context(tc.psum_pool(name="psum_o", bufs=2))
         stack.enter_context(tc.manual_schedule())
@@ -367,6 +368,21 @@ def tile_refphi4flashdiffattention_pa_t_kernel(
                 in_=y[:],
             )
 
+        def filler(j):
+            if not 0 <= j < N_HALF:
+                return
+            v_codes, v_scales = v_mx[j // 4]
+            idle = psum_x.tile([P, S], F32, name="idle")
+            nc.tensor.matmul_mx(
+                out=idle[:],
+                lhsT=v_codes[:, 0:P].bitcast(FP8X4),
+                lhsT_scale=v_scales[:, 0:P],
+                rhs=v_codes[:].bitcast(FP8X4),
+                rhs_scale=v_scales[:],
+                start=True,
+                stop=True,
+            )
+
         load_batch(0)
         load_small()
         load_batch(1)
@@ -376,6 +392,7 @@ def tile_refphi4flashdiffattention_pa_t_kernel(
             if j >= 0 and j % 4 == 0:
                 load_batch(j // 4 + 2)
             mx_passes(j - 2)
+            filler(j)
             score_matmuls(j, 1)
             sum_squares(j - 3, 1)
             exponentials(j - 1, 3)
@@ -385,6 +402,7 @@ def tile_refphi4flashdiffattention_pa_t_kernel(
             copy_e_words(j - 1, 0)
             finish(j - 3)
             scale_second(j - 2, 0)
+            filler(j)
             score_matmuls(j, 2)
             transpose_e(j - 1, 1)
             if starts_unit:
@@ -397,6 +415,7 @@ def tile_refphi4flashdiffattention_pa_t_kernel(
                 regroup_v((j + 2) // 4)
             if (j + 1) % 4 == 0:
                 quantise_v((j + 1) // 4)
+            filler(j)
             score_matmuls(j, 3)
             copy_e_words(j - 1, 1)
             if starts_unit:
@@ -405,6 +424,7 @@ def tile_refphi4flashdiffattention_pa_t_kernel(
             exponentials(j, 1)
             exponentials(j, 2)
             quantise_e(j - 1, 0)
+            filler(j)
             score_matmuls(j + 1, 0)
             difference(j - 2, 0)
             difference(j - 2, 1)

@@ -39,8 +39,7 @@ def tile_refphi4flashdiffattention_pa_t_kernel(
         work = stack.enter_context(tc.tile_pool(name="work", bufs=4))
         stats = stack.enter_context(tc.tile_pool(name="stats", bufs=6))
         psum_tp = stack.enter_context(tc.psum_pool(name="psum_tp", bufs=1))
-        psum_s = stack.enter_context(tc.psum_pool(name="psum_s", bufs=2))
-        psum_x = stack.enter_context(tc.psum_pool(name="psum_x", bufs=1))
+        psum_s = stack.enter_context(tc.psum_pool(name="psum_s", bufs=3))
         psum_et = stack.enter_context(tc.psum_pool(name="psum_et", bufs=2))
         psum_o = stack.enter_context(tc.psum_pool(name="psum_o", bufs=2))
         stack.enter_context(tc.manual_schedule())
@@ -94,6 +93,7 @@ def tile_refphi4flashdiffattention_pa_t_kernel(
         seconds = {}
         xs = {}
         mean_sqs = {}
+        gained = {}
 
         def load_batch(b):
             if b >= B:
@@ -337,7 +337,6 @@ def tile_refphi4flashdiffattention_pa_t_kernel(
         def finish(j):
             if not 0 <= j < N_HALF:
                 return
-            b, pr, g = j // 4, (j // 2) % PAIRS, j % 2
             xg = work.tile([P, 2, 2 * D], F32, name="xg")
             nc.gpsimd.tensor_tensor(
                 out=xg[:],
@@ -351,36 +350,27 @@ def tile_refphi4flashdiffattention_pa_t_kernel(
             )
             rstd = stats.tile([P, 2], F32, name="rstd")
             nc.gpsimd.tensor_tensor(out=rstd[:], in0=var_eps[:], in1=neg_half[:], op=ALU.pow)
+            gained[j] = (xg, rstd)
+
+        def scale_and_store(j):
+            if not 0 <= j < N_HALF:
+                return
+            b, pr, g = j // 4, (j // 2) % PAIRS, j % 2
+            xg, rstd = gained[j]
             y = work.tile([P, 2, 2 * D], F32, name="y")
             for ii in range(2):
-                nc.gpsimd.tensor_scalar(
+                nc.vector.tensor_scalar(
                     out=y[:, ii, :],
                     in0=xg[:, ii, :],
                     scalar1=rstd[:, ii : ii + 1],
-                    scalar2=0.0,
+                    scalar2=None,
                     op0=ALU.mult,
-                    op1=ALU.add,
                 )
             nc.sync.dma_start(
                 out=out[b, g * 2 * P : (g + 1) * 2 * P, 2 * pr : 2 * pr + 2, :].rearrange(
                     "(i p) h d -> p i (h d)", p=P
                 ),
                 in_=y[:],
-            )
-
-        def filler(j):
-            if not 0 <= j < N_HALF:
-                return
-            v_codes, v_scales = v_mx[j // 4]
-            idle = psum_x.tile([P, S], F32, name="idle")
-            nc.tensor.matmul_mx(
-                out=idle[:],
-                lhsT=v_codes[:, 0:P].bitcast(FP8X4),
-                lhsT_scale=v_scales[:, 0:P],
-                rhs=v_codes[:].bitcast(FP8X4),
-                rhs_scale=v_scales[:],
-                start=True,
-                stop=True,
             )
 
         load_batch(0)
@@ -392,7 +382,6 @@ def tile_refphi4flashdiffattention_pa_t_kernel(
             if j >= 0 and j % 4 == 0:
                 load_batch(j // 4 + 2)
             mx_passes(j - 2)
-            filler(j)
             score_matmuls(j, 1)
             sum_squares(j - 3, 1)
             exponentials(j - 1, 3)
@@ -402,7 +391,6 @@ def tile_refphi4flashdiffattention_pa_t_kernel(
             copy_e_words(j - 1, 0)
             finish(j - 3)
             scale_second(j - 2, 0)
-            filler(j)
             score_matmuls(j, 2)
             transpose_e(j - 1, 1)
             if starts_unit:
@@ -415,7 +403,6 @@ def tile_refphi4flashdiffattention_pa_t_kernel(
                 regroup_v((j + 2) // 4)
             if (j + 1) % 4 == 0:
                 quantise_v((j + 1) // 4)
-            filler(j)
             score_matmuls(j, 3)
             copy_e_words(j - 1, 1)
             if starts_unit:
@@ -424,7 +411,6 @@ def tile_refphi4flashdiffattention_pa_t_kernel(
             exponentials(j, 1)
             exponentials(j, 2)
             quantise_e(j - 1, 0)
-            filler(j)
             score_matmuls(j + 1, 0)
             difference(j - 2, 0)
             difference(j - 2, 1)
@@ -436,3 +422,4 @@ def tile_refphi4flashdiffattention_pa_t_kernel(
             if starts_unit:
                 copy_qk(next_unit, 1)
             quantise_e(j - 1, 1)
+            scale_and_store(j - 3)

@@ -93,7 +93,6 @@ def tile_refphi4flashdiffattention_pa_t_kernel(
         seconds = {}
         xs = {}
         mean_sqs = {}
-        gained = {}
 
         def load_batch(b):
             if b >= B:
@@ -246,10 +245,7 @@ def tile_refphi4flashdiffattention_pa_t_kernel(
             e_grouped = work.tile([P, 2 * P * PACK], BF16, name="e_grouped", align_bytes=64)
             dst = e_grouped[:].bitcast(F32).rearrange("p (i q u) -> p i q u", i=2, u=2)
             src = word_banks[(j, hh)][:].rearrange("p i u q -> p i q u")
-            if hh == 0:
-                nc.vector.tensor_copy(out=dst, in_=src)
-            else:
-                nc.scalar.copy(out=dst, in_=src)
+            nc.scalar.copy(out=dst, in_=src)
             grouped[(j, hh)] = e_grouped
 
         def quantise_e(j, hh):
@@ -337,6 +333,7 @@ def tile_refphi4flashdiffattention_pa_t_kernel(
         def finish(j):
             if not 0 <= j < N_HALF:
                 return
+            b, pr, g = j // 4, (j // 2) % PAIRS, j % 2
             xg = work.tile([P, 2, 2 * D], F32, name="xg")
             nc.gpsimd.tensor_tensor(
                 out=xg[:],
@@ -350,21 +347,15 @@ def tile_refphi4flashdiffattention_pa_t_kernel(
             )
             rstd = stats.tile([P, 2], F32, name="rstd")
             nc.gpsimd.tensor_tensor(out=rstd[:], in0=var_eps[:], in1=neg_half[:], op=ALU.pow)
-            gained[j] = (xg, rstd)
-
-        def scale_and_store(j):
-            if not 0 <= j < N_HALF:
-                return
-            b, pr, g = j // 4, (j // 2) % PAIRS, j % 2
-            xg, rstd = gained[j]
             y = work.tile([P, 2, 2 * D], F32, name="y")
             for ii in range(2):
-                nc.vector.tensor_scalar(
+                nc.gpsimd.tensor_scalar(
                     out=y[:, ii, :],
                     in0=xg[:, ii, :],
                     scalar1=rstd[:, ii : ii + 1],
-                    scalar2=None,
+                    scalar2=0.0,
                     op0=ALU.mult,
+                    op1=ALU.add,
                 )
             nc.sync.dma_start(
                 out=out[b, g * 2 * P : (g + 1) * 2 * P, 2 * pr : 2 * pr + 2, :].rearrange(
@@ -422,4 +413,3 @@ def tile_refphi4flashdiffattention_pa_t_kernel(
             if starts_unit:
                 copy_qk(next_unit, 1)
             quantise_e(j - 1, 1)
-            scale_and_store(j - 3)

@@ -24,7 +24,10 @@ NEG_INF = -1e30
 EPS = 1e-5
 SCALE = 1.0 / math.sqrt(D)
 E_SLOTS = 2
-N_HALF = B * PAIRS * 2
+N_HEADS = B * H
+N_UNITS = B * PAIRS
+N_HALF = 2 * N_UNITS
+N_TILES = 4 * N_HALF
 
 FLOPS = 2 * B * H * S * S * D + 2 * B * H * S * S * 2 * D
 
@@ -37,7 +40,7 @@ def tile_refphi4flashdiffattention_pa_t_kernel(
         const = stack.enter_context(tc.tile_pool(name="const", bufs=1))
         loads = stack.enter_context(tc.tile_pool(name="loads", bufs=3))
         work = stack.enter_context(tc.tile_pool(name="work", bufs=4))
-        stats = stack.enter_context(tc.tile_pool(name="stats", bufs=6))
+        stats = stack.enter_context(tc.tile_pool(name="stats", bufs=4))
         psum_tp = stack.enter_context(tc.psum_pool(name="psum_tp", bufs=1))
         psum_s = stack.enter_context(tc.psum_pool(name="psum_s", bufs=3))
         psum_et = stack.enter_context(tc.psum_pool(name="psum_et", bufs=2))
@@ -75,53 +78,63 @@ def tile_refphi4flashdiffattention_pa_t_kernel(
 
         lam_in = const.tile([P, 4, D], BF16, name="lam_in")
         w_in = const.tile([P, 2 * D], BF16, name="w_in")
+        dots = const.tile([P, 2], F32, name="dots")
+        exps = const.tile([P, 2], F32, name="exps")
         lam = const.tile([P, 1], F32, name="lam")
         gain = const.tile([P, 2 * D], F32, name="gain")
 
         inputs = {}
+        v_grouped = {}
         v_mx = {}
         qk_banks = {}
         qk_t = {}
         score_banks = {}
         scores = {}
         rowsums = {}
+        invs = {}
+        lam_invs = {}
         word_banks = {}
-        grouped = {}
+        e_grouped = {}
         e_mx = {}
-        factors = {}
         out_banks = {}
         seconds = {}
         xs = {}
         mean_sqs = {}
 
-        def load_batch(b):
-            if b >= B:
-                return
+        def load_qk(b):
             q_sb = loads.tile([P, QT, H * D], BF16, name="q_sb")
             nc.sync.dma_start(out=q_sb[:], in_=q[b].rearrange("(t p) h d -> p t (h d)", p=P))
             k_sb = loads.tile([P, QT, H * D], BF16, name="k_sb")
             nc.sync.dma_start(out=k_sb[:], in_=k[b].rearrange("(t p) h d -> p t (h d)", p=P))
+            inputs[b] = (q_sb, k_sb)
+
+        def load_v(b):
             v_sb = loads.tile([P, PACK, H * D], BF16, name="v_sb")
             nc.sync.dma_start(
                 out=v_sb[:].rearrange("p (u e) f -> p u (e f)", u=2),
                 in_=v[b].rearrange("(u p e) h d -> p u (e h d)", u=2, e=2),
             )
-            inputs[b] = (q_sb, k_sb, v_sb)
+            inputs[("v", b)] = v_sb
 
         def load_small():
             for c, vec in enumerate((lambda_q1, lambda_q2, lambda_k1, lambda_k2)):
                 nc.sync.dma_start(out=lam_in[:, c, :], in_=vec.partition_broadcast(P))
             nc.sync.dma_start(out=w_in[:], in_=subln_weight.partition_broadcast(P))
 
-        def lam_and_gain():
+        def lam_dots_and_gain():
             prod = const.tile([P, 2, D], F32, name="prod")
             nc.vector.tensor_tensor(
                 out=prod[:], in0=lam_in[:, 0:2, :], in1=lam_in[:, 2:4, :], op=ALU.mult
             )
-            dots = const.tile([P, 2], F32, name="dots")
+            nc.vector.tensor_scalar(
+                out=gain[:], in0=w_in[:], scalar1=1.0 - LAMBDA_INIT, scalar2=None, op0=ALU.mult
+            )
             nc.vector.tensor_reduce(out=dots[:], in_=prod[:], axis=AXIS_X, op=ALU.add)
-            exps = const.tile([P, 2], F32, name="exps")
+
+        def lam_exps():
             nc.scalar.activation(out=exps[:], in_=dots[:], func=ACT.Exp)
+
+        def lam_value():
             nc.vector.tensor_scalar(
                 out=lam[:],
                 in0=exps[:, 0:1],
@@ -130,59 +143,58 @@ def tile_refphi4flashdiffattention_pa_t_kernel(
                 op0=ALU.subtract,
                 op1=ALU.add,
             )
-            nc.vector.tensor_scalar(
-                out=gain[:], in0=w_in[:], scalar1=1.0 - LAMBDA_INIT, scalar2=None, op0=ALU.mult
-            )
 
         def regroup_v(b):
-            if b >= B:
+            if not 0 <= b < B:
                 return
-            v_sb = inputs[b][2]
-            v_grouped = work.tile([P, H * D, PACK], BF16, name="v_grouped", bufs=2, align_bytes=64)
+            grouped = work.tile([P, H * D, PACK], BF16, name="v_grouped", bufs=2, align_bytes=64)
             nc.vector.tensor_copy(
-                out=v_grouped[:].rearrange("p (c i) t -> p c t i", i=4),
-                in_=v_sb[:].rearrange("p t (c i) -> p c t i", i=4),
+                out=grouped[:].rearrange("p (c i) t -> p c t i", i=4),
+                in_=inputs[("v", b)][:].rearrange("p t (c i) -> p c t i", i=4),
             )
-            grouped[("v", b)] = v_grouped
+            v_grouped[b] = grouped
 
         def quantise_v(b):
-            if b >= B:
+            if not 0 <= b < B:
                 return
             v_codes = work.tile([P, H * D], U32, name="v_codes", bufs=3, align_bytes=64)
             v_scales = work.tile([P, H * D], U8, name="v_scales", bufs=3, align_bytes=64)
             nc.vector.quantize_mx(
                 out=v_codes[:].bitcast(FP8X4),
                 scales=v_scales[:],
-                in_=grouped[("v", b)][:].rearrange("p f t -> p (f t)"),
+                in_=v_grouped[b][:].rearrange("p f t -> p (f t)"),
             )
             v_mx[b] = (v_codes, v_scales)
 
-        def transpose_qk(unit, hh):
-            if unit >= B * PAIRS:
+        def transpose_qk(h):
+            if not 0 <= h < N_HEADS:
                 return
-            q_sb, k_sb = inputs[unit // PAIRS][0:2]
-            h = 2 * (unit % PAIRS) + hh
-            head_cols = slice(h * D, (h + 1) * D)
+            q_sb, k_sb = inputs[h // H]
+            head_cols = slice((h % H) * D, (h % H + 1) * D)
             tp = psum_tp.tile([P, 2 * QT, P], BF16, name="tp")
             for t in range(QT):
                 nc.tensor.transpose(tp[:, t, :], q_sb[:, t, head_cols], ident_bf[:])
             for t in range(QT):
                 nc.tensor.transpose(tp[:, QT + t, :], k_sb[:, t, head_cols], ident_bf[:])
-            qk_banks[(unit, hh)] = tp
+            qk_banks[h] = tp
 
-        def copy_qk(unit, hh):
-            if unit >= B * PAIRS:
+        def copy_qk(h):
+            if not 0 <= h < N_HEADS:
                 return
             qk = work.tile([P, 2 * S], BF16, name="qk", bufs=6)
-            nc.scalar.copy(out=qk[:], in_=qk_banks[(unit, hh)][:].rearrange("p t c -> p (t c)"))
-            qk_t[(unit, hh)] = qk
+            nc.scalar.copy(out=qk[:], in_=qk_banks[h][:].rearrange("p t c -> p (t c)"))
+            qk_t[h] = qk
 
-        def score_matmuls(j, tau):
-            if not 0 <= j < N_HALF:
+        def tile_place(n):
+            j, tau = divmod(n, 4)
+            return j, tau // 2, 2 * (j % 2) + tau % 2
+
+        def score_matmuls(n):
+            if not 0 <= n < N_TILES:
                 return
-            hh, i = tau // 2, 2 * (j % 2) + tau % 2
-            q_t = qk_t[(j // 2, hh)][:, 0:S]
-            k_t = qk_t[(j // 2, hh)][:, S : 2 * S]
+            j, hh, i = tile_place(n)
+            q_t = qk_t[2 * (j // 2) + hh][:, 0:S]
+            k_t = qk_t[2 * (j // 2) + hh][:, S : 2 * S]
             own = slice(i * P, (i + 1) * P)
             s_ps = psum_s.tile([P, S], F32, name="s_ps")
             nc.tensor.matmul(s_ps[:, own], lhsT=ident_bf[:], rhs=mask_bf[:], start=True, stop=False)
@@ -191,40 +203,40 @@ def tile_refphi4flashdiffattention_pa_t_kernel(
                 nc.tensor.matmul(
                     s_ps[:, 0 : i * P], lhsT=q_t[:, own], rhs=k_t[:, 0 : i * P], start=True, stop=True
                 )
-            score_banks[(j, tau)] = s_ps
+            score_banks[n] = s_ps
 
-        def row_maximum(j, tau):
-            if not 0 <= j < N_HALF:
+        def row_maximum(n):
+            if not 0 <= n < N_TILES:
                 return
-            n = (2 * (j % 2) + tau % 2 + 1) * P
-            s_sb = work.tile([P, S], F32, name="s_sb")
-            shift = stats.tile([P, 1], F32, name="shift")
+            width = (tile_place(n)[2] + 1) * P
+            s_sb = work.tile([P, S], F32, name="s_sb", bufs=8)
+            shift = stats.tile([P, 1], F32, name="shift", bufs=8)
             nc.vector.tensor_scalar(
-                out=s_sb[:, 0:n],
-                in0=score_banks[(j, tau)][:, 0:n],
+                out=s_sb[:, 0:width],
+                in0=score_banks[n][:, 0:width],
                 scalar1=-SCALE,
                 scalar2=None,
                 op0=ALU.mult,
                 op1=ALU.min,
                 accum_out=shift[:],
             )
-            scores[(j, tau)] = (s_sb, shift)
+            scores[n] = (s_sb, shift)
 
-        def exponentials(j, tau):
-            if not 0 <= j < N_HALF:
+        def exponentials(n):
+            if not 0 <= n < N_TILES:
                 return
-            hh, i = tau // 2, 2 * (j % 2) + tau % 2
-            n = (i + 1) * P
-            if tau == 0:
-                rowsums[j] = stats.tile([P, 4], F32, name="rowsum")
-            s_sb, shift = scores[(j, tau)]
+            j, hh, i = tile_place(n)
+            width = (i + 1) * P
+            if n % 8 == 0:
+                rowsums[j // 2] = stats.tile([P, 2 * QT], F32, name="rowsum")
+            s_sb, shift = scores[n]
             nc.scalar.activation(
-                out=e_tiles[((j // 2) % E_SLOTS, hh, i)][:, 0:n],
-                in_=s_sb[:, 0:n],
+                out=e_tiles[((j // 2) % E_SLOTS, hh, i)][:, 0:width],
+                in_=s_sb[:, 0:width],
                 func=ACT.Exp,
                 bias=shift[:],
                 scale=-1.0,
-                accum_out=rowsums[j][:, tau : tau + 1],
+                accum_out=rowsums[j // 2][:, QT * hh + i : QT * hh + i + 1],
             )
 
         def transpose_e(j, hh):
@@ -242,36 +254,37 @@ def tile_refphi4flashdiffattention_pa_t_kernel(
         def copy_e_words(j, hh):
             if not 0 <= j < N_HALF:
                 return
-            e_grouped = work.tile([P, 2 * P * PACK], BF16, name="e_grouped", align_bytes=64)
-            dst = e_grouped[:].bitcast(F32).rearrange("p (i q u) -> p i q u", i=2, u=2)
-            src = word_banks[(j, hh)][:].rearrange("p i u q -> p i q u")
-            nc.scalar.copy(out=dst, in_=src)
-            grouped[(j, hh)] = e_grouped
+            if hh == 0:
+                e_grouped[j] = work.tile([P, 2, 2 * P * PACK], BF16, name="e_grouped", align_bytes=64)
+            dst = e_grouped[j][:, hh, :].bitcast(F32).rearrange("p (i q u) -> p i q u", i=2, u=2)
+            nc.scalar.copy(out=dst, in_=word_banks[(j, hh)][:].rearrange("p i u q -> p i q u"))
 
-        def quantise_e(j, hh):
+        def quantise_e(j):
             if not 0 <= j < N_HALF:
                 return
-            codes = work.tile([P, 2 * P], U32, name="codes", bufs=6, align_bytes=64)
-            scales = work.tile([P, 2 * P], U8, name="scales", bufs=6, align_bytes=64)
+            codes = work.tile([P, 2, 2 * P], U32, name="codes", align_bytes=64)
+            scales = work.tile([P, 2, 2 * P], U8, name="scales", align_bytes=64)
             nc.vector.quantize_mx(
-                out=codes[:].bitcast(FP8X4), scales=scales[:], in_=grouped[(j, hh)][:]
+                out=codes[:].rearrange("p h c -> p (h c)").bitcast(FP8X4),
+                scales=scales[:].rearrange("p h c -> p (h c)"),
+                in_=e_grouped[j][:].rearrange("p h c -> p (h c)"),
             )
-            e_mx[(j, hh)] = (codes, scales)
+            e_mx[j] = (codes, scales)
 
         def mx_passes(j):
             if not 0 <= j < N_HALF:
                 return
             v_codes, v_scales = v_mx[j // 4]
+            codes, scales = e_mx[j]
             pair_cols = slice(((j // 2) % PAIRS) * 2 * D, ((j // 2) % PAIRS + 1) * 2 * D)
             for ii in range(2):
                 q_cols = slice(ii * P, (ii + 1) * P)
                 o_ps = psum_o.tile([P, 2, 2 * D], F32, name="o_ps")
                 for hh in range(2):
-                    codes, scales = e_mx[(j, hh)]
                     nc.tensor.matmul_mx(
                         out=o_ps[:, hh, :],
-                        lhsT=codes[:, q_cols].bitcast(FP8X4),
-                        lhsT_scale=scales[:, q_cols],
+                        lhsT=codes[:, hh, q_cols].bitcast(FP8X4),
+                        lhsT_scale=scales[:, hh, q_cols],
                         rhs=v_codes[:, pair_cols].bitcast(FP8X4),
                         rhs_scale=v_scales[:, pair_cols],
                         start=True,
@@ -279,38 +292,45 @@ def tile_refphi4flashdiffattention_pa_t_kernel(
                     )
                 out_banks[(j, ii)] = o_ps
 
-        def normalisers(j):
-            if not 0 <= j < N_HALF:
+        def reciprocals(unit):
+            if not 0 <= unit < N_UNITS:
                 return
-            inv = stats.tile([P, 4], F32, name="inv")
-            nc.vector.reciprocal(out=inv[:], in_=rowsums[j][:])
-            lam_inv = stats.tile([P, 2], F32, name="lam_inv")
+            inv = stats.tile([P, 2 * QT], F32, name="inv")
+            nc.vector.reciprocal(out=inv[:], in_=rowsums[unit][:])
+            invs[unit] = inv
+
+        def times_lam(unit):
+            if not 0 <= unit < N_UNITS:
+                return
+            lam_inv = stats.tile([P, QT], F32, name="lam_inv")
             nc.vector.tensor_scalar(
-                out=lam_inv[:], in0=inv[:, 2:4], scalar1=lam[:], scalar2=None, op0=ALU.mult
+                out=lam_inv[:], in0=invs[unit][:, QT : 2 * QT], scalar1=lam[:], scalar2=None, op0=ALU.mult
             )
-            factors[j] = (inv, lam_inv)
+            lam_invs[unit] = lam_inv
 
         def scale_second(j, ii):
             if not 0 <= j < N_HALF:
                 return
+            i = 2 * (j % 2) + ii
             second = work.tile([P, 2 * D], F32, name="second")
             nc.scalar.activation(
                 out=second[:],
                 in_=out_banks[(j, ii)][:, 1, :],
                 func=ACT.Copy,
-                scale=factors[j][1][:, ii : ii + 1],
+                scale=lam_invs[j // 2][:, i : i + 1],
             )
             seconds[(j, ii)] = second
 
         def difference(j, ii):
             if not 0 <= j < N_HALF:
                 return
+            i = 2 * (j % 2) + ii
             if ii == 0:
-                xs[j] = work.tile([P, 2, 2 * D], F32, name="x")
+                xs[j] = work.tile([P, 2, 2 * D], F32, name="x", bufs=5)
             nc.vector.scalar_tensor_tensor(
                 out=xs[j][:, ii, :],
                 in0=out_banks[(j, ii)][:, 0, :],
-                scalar=factors[j][0][:, ii : ii + 1],
+                scalar=invs[j // 2][:, i : i + 1],
                 in1=seconds[(j, ii)][:],
                 op0=ALU.mult,
                 op1=ALU.subtract,
@@ -334,16 +354,16 @@ def tile_refphi4flashdiffattention_pa_t_kernel(
             if not 0 <= j < N_HALF:
                 return
             b, pr, g = j // 4, (j // 2) % PAIRS, j % 2
+            var_eps = stats.tile([P, 2], F32, name="var_eps")
+            nc.gpsimd.tensor_scalar(
+                out=var_eps[:], in0=mean_sqs[j][:], scalar1=1.0, scalar2=EPS, op0=ALU.mult, op1=ALU.add
+            )
             xg = work.tile([P, 2, 2 * D], F32, name="xg")
             nc.gpsimd.tensor_tensor(
                 out=xg[:],
                 in0=xs[j][:],
                 in1=gain[:].unsqueeze(1).to_broadcast([P, 2, 2 * D]),
                 op=ALU.mult,
-            )
-            var_eps = stats.tile([P, 2], F32, name="var_eps")
-            nc.gpsimd.tensor_scalar(
-                out=var_eps[:], in0=mean_sqs[j][:], scalar1=1.0, scalar2=EPS, op0=ALU.mult, op1=ALU.add
             )
             rstd = stats.tile([P, 2], F32, name="rstd")
             nc.gpsimd.tensor_tensor(out=rstd[:], in0=var_eps[:], in1=neg_half[:], op=ALU.pow)
@@ -364,52 +384,53 @@ def tile_refphi4flashdiffattention_pa_t_kernel(
                 in_=y[:],
             )
 
-        load_batch(0)
+        load_qk(0)
         load_small()
-        load_batch(1)
-        for j in range(-2, N_HALF + 3):
-            starts_unit = (j + 1) % 2 == 0
-            next_unit = (j + 1) // 2
-            if j >= 0 and j % 4 == 0:
-                load_batch(j // 4 + 2)
-            mx_passes(j - 2)
-            score_matmuls(j, 1)
-            sum_squares(j - 3, 1)
-            exponentials(j - 1, 3)
-            row_maximum(j, 0)
-            exponentials(j, 0)
-            normalisers(j - 2)
-            copy_e_words(j - 1, 0)
-            finish(j - 3)
-            scale_second(j - 2, 0)
-            score_matmuls(j, 2)
-            transpose_e(j - 1, 1)
-            if starts_unit:
-                transpose_qk(next_unit, 0)
-            scale_second(j - 2, 1)
-            row_maximum(j, 1)
-            if j == 0:
-                lam_and_gain()
-            if (j + 2) % 4 == 0:
-                regroup_v((j + 2) // 4)
-            if (j + 1) % 4 == 0:
-                quantise_v((j + 1) // 4)
-            score_matmuls(j, 3)
-            copy_e_words(j - 1, 1)
-            if starts_unit:
-                copy_qk(next_unit, 0)
-            row_maximum(j, 2)
-            exponentials(j, 1)
-            exponentials(j, 2)
-            quantise_e(j - 1, 0)
-            score_matmuls(j + 1, 0)
-            difference(j - 2, 0)
-            difference(j - 2, 1)
-            if starts_unit:
-                transpose_qk(next_unit, 1)
-            transpose_e(j, 0)
-            sum_squares(j - 2, 0)
-            row_maximum(j, 3)
-            if starts_unit:
-                copy_qk(next_unit, 1)
-            quantise_e(j - 1, 1)
+        load_v(0)
+        load_qk(1)
+        load_v(1)
+        lam_dots_and_gain()
+        for r in range(-3, N_HALF + 8):
+            first = 4 * r
+            if r >= 0 and r % 4 == 0 and r // 4 + 2 < B:
+                load_qk(r // 4 + 2)
+                load_v(r // 4 + 2)
+            score_matmuls(first + 2)
+            mx_passes(r - 5)
+            exponentials(first - 4)
+            row_maximum(first)
+            copy_qk(r + 2)
+            sum_squares(r - 7, 1)
+            score_matmuls(first + 3)
+            transpose_e(r - 2, 0)
+            exponentials(first - 3)
+            row_maximum(first + 1)
+            copy_e_words(r - 3, 1)
+            quantise_e(r - 4)
+            if r % 2 == 1:
+                reciprocals((r - 3) // 2)
+            if r == 0:
+                lam_exps()
+            score_matmuls(first + 4)
+            transpose_qk(r + 3)
+            exponentials(first - 2)
+            row_maximum(first + 2)
+            scale_second(r - 5, 0)
+            scale_second(r - 5, 1)
+            if r % 4 == 1:
+                regroup_v(r // 4)
+            if r % 4 == 2:
+                quantise_v(r // 4)
+            if r == 1:
+                lam_value()
+            if r % 2 == 1:
+                times_lam((r - 3) // 2)
+            score_matmuls(first + 5)
+            transpose_e(r - 2, 1)
+            exponentials(first - 1)
+            row_maximum(first + 3)
+            sum_squares(r - 6, 0)
+            copy_e_words(r - 2, 0)
+            difference(r - 5, 0)
+            difference(r - 5, 1)
+            finish(r - 7)

@@ -28,6 +28,7 @@ N_HEADS = B * H
 N_UNITS = B * PAIRS
 N_HALF = 2 * N_UNITS
 N_TILES = 4 * N_HALF
+TAIL = 4
 
 FLOPS = 2 * B * H * S * S * D + 2 * B * H * S * S * 2 * D
 
@@ -182,7 +183,7 @@ def tile_refphi4flashdiffattention_pa_t_kernel(
             if not 0 <= h < N_HEADS:
                 return
             qk = work.tile([P, 2 * S], BF16, name="qk", bufs=6)
-            nc.scalar.copy(out=qk[:], in_=qk_banks[h][:].rearrange("p t c -> p (t c)"))
+            nc.vector.tensor_copy(out=qk[:], in_=qk_banks[h][:].rearrange("p t c -> p (t c)"))
             qk_t[h] = qk
 
         def tile_place(n):
@@ -354,29 +355,41 @@ def tile_refphi4flashdiffattention_pa_t_kernel(
             if not 0 <= j < N_HALF:
                 return
             b, pr, g = j // 4, (j // 2) % PAIRS, j % 2
+            on_gpsimd = j < N_HALF - TAIL
+            if on_gpsimd:
+                xg = work.tile([P, 2, 2 * D], F32, name="xg")
+                nc.gpsimd.tensor_tensor(
+                    out=xg[:],
+                    in0=xs[j][:],
+                    in1=gain[:].unsqueeze(1).to_broadcast([P, 2, 2 * D]),
+                    op=ALU.mult,
+                )
             var_eps = stats.tile([P, 2], F32, name="var_eps")
             nc.gpsimd.tensor_scalar(
                 out=var_eps[:], in0=mean_sqs[j][:], scalar1=1.0, scalar2=EPS, op0=ALU.mult, op1=ALU.add
-            )
-            xg = work.tile([P, 2, 2 * D], F32, name="xg")
-            nc.gpsimd.tensor_tensor(
-                out=xg[:],
-                in0=xs[j][:],
-                in1=gain[:].unsqueeze(1).to_broadcast([P, 2, 2 * D]),
-                op=ALU.mult,
             )
             rstd = stats.tile([P, 2], F32, name="rstd")
             nc.gpsimd.tensor_tensor(out=rstd[:], in0=var_eps[:], in1=neg_half[:], op=ALU.pow)
             y = work.tile([P, 2, 2 * D], F32, name="y")
             for ii in range(2):
-                nc.gpsimd.tensor_scalar(
-                    out=y[:, ii, :],
-                    in0=xg[:, ii, :],
-                    scalar1=rstd[:, ii : ii + 1],
-                    scalar2=0.0,
-                    op0=ALU.mult,
-                    op1=ALU.add,
-                )
+                if on_gpsimd:
+                    nc.gpsimd.tensor_scalar(
+                        out=y[:, ii, :],
+                        in0=xg[:, ii, :],
+                        scalar1=rstd[:, ii : ii + 1],
+                        scalar2=0.0,
+                        op0=ALU.mult,
+                        op1=ALU.add,
+                    )
+                else:
+                    nc.vector.scalar_tensor_tensor(
+                        out=y[:, ii, :],
+                        in0=xs[j][:, ii, :],
+                        scalar=rstd[:, ii : ii + 1],
+                        in1=gain[:],
+                        op0=ALU.mult,
+                        op1=ALU.mult,
+                    )
             nc.sync.dma_start(
                 out=out[b, g * 2 * P : (g + 1) * 2 * P, 2 * pr : 2 * pr + 2, :].rearrange(
                     "(i p) h d -> p i (h d)", p=P

@@ -183,7 +183,10 @@ def tile_refphi4flashdiffattention_pa_t_kernel(
             if not 0 <= h < N_HEADS:
                 return
             qk = work.tile([P, 2 * S], BF16, name="qk", bufs=6)
-            nc.vector.tensor_copy(out=qk[:], in_=qk_banks[h][:].rearrange("p t c -> p (t c)"))
+            if h % 2 == 0:
+                nc.vector.tensor_copy(out=qk[:], in_=qk_banks[h][:].rearrange("p t c -> p (t c)"))
+            else:
+                nc.scalar.copy(out=qk[:], in_=qk_banks[h][:].rearrange("p t c -> p (t c)"))
             qk_t[h] = qk
 
         def tile_place(n):

@@ -23,11 +23,12 @@ LAMBDA_INIT = 0.8 - 0.6 * math.exp(-0.3 * DEPTH)
 NEG_INF = -1e30
 EPS = 1e-5
 SCALE = 1.0 / math.sqrt(D)
-E_SLOTS = 2
+
 N_HEADS = B * H
 N_UNITS = B * PAIRS
 N_HALF = 2 * N_UNITS
 N_TILES = 4 * N_HALF
+E_SLOTS = 2
 TAIL = 4
 
 FLOPS = 2 * B * H * S * S * D + 2 * B * H * S * S * 2 * D
@@ -84,7 +85,8 @@ def tile_refphi4flashdiffattention_pa_t_kernel(
         lam = const.tile([P, 1], F32, name="lam")
         gain = const.tile([P, 2 * D], F32, name="gain")
 
-        inputs = {}
+        qk_inputs = {}
+        v_inputs = {}
         v_grouped = {}
         v_mx = {}
         qk_banks = {}
@@ -101,13 +103,15 @@ def tile_refphi4flashdiffattention_pa_t_kernel(
         seconds = {}
         xs = {}
         mean_sqs = {}
+        gained = {}
+        rstds = {}
 
         def load_qk(b):
             q_sb = loads.tile([P, QT, H * D], BF16, name="q_sb")
             nc.sync.dma_start(out=q_sb[:], in_=q[b].rearrange("(t p) h d -> p t (h d)", p=P))
             k_sb = loads.tile([P, QT, H * D], BF16, name="k_sb")
             nc.sync.dma_start(out=k_sb[:], in_=k[b].rearrange("(t p) h d -> p t (h d)", p=P))
-            inputs[b] = (q_sb, k_sb)
+            qk_inputs[b] = (q_sb, k_sb)
 
         def load_v(b):
             v_sb = loads.tile([P, PACK, H * D], BF16, name="v_sb")
@@ -115,7 +119,7 @@ def tile_refphi4flashdiffattention_pa_t_kernel(
                 out=v_sb[:].rearrange("p (u e) f -> p u (e f)", u=2),
                 in_=v[b].rearrange("(u p e) h d -> p u (e h d)", u=2, e=2),
             )
-            inputs[("v", b)] = v_sb
+            v_inputs[b] = v_sb
 
         def load_small():
             for c, vec in enumerate((lambda_q1, lambda_q2, lambda_k1, lambda_k2)):
@@ -151,7 +155,7 @@ def tile_refphi4flashdiffattention_pa_t_kernel(
             grouped = work.tile([P, H * D, PACK], BF16, name="v_grouped", bufs=2, align_bytes=64)
             nc.vector.tensor_copy(
                 out=grouped[:].rearrange("p (c i) t -> p c t i", i=4),
-                in_=inputs[("v", b)][:].rearrange("p t (c i) -> p c t i", i=4),
+                in_=v_inputs[b][:].rearrange("p t (c i) -> p c t i", i=4),
             )
             v_grouped[b] = grouped
 
@@ -170,7 +174,7 @@ def tile_refphi4flashdiffattention_pa_t_kernel(
         def transpose_qk(h):
             if not 0 <= h < N_HEADS:
                 return
-            q_sb, k_sb = inputs[h // H]
+            q_sb, k_sb = qk_inputs[h // H]
             head_cols = slice((h % H) * D, (h % H + 1) * D)
             tp = psum_tp.tile([P, 2 * QT, P], BF16, name="tp")
             for t in range(QT):
@@ -183,10 +187,7 @@ def tile_refphi4flashdiffattention_pa_t_kernel(
             if not 0 <= h < N_HEADS:
                 return
             qk = work.tile([P, 2 * S], BF16, name="qk", bufs=6)
-            if h % 2 == 0:
-                nc.vector.tensor_copy(out=qk[:], in_=qk_banks[h][:].rearrange("p t c -> p (t c)"))
-            else:
-                nc.scalar.copy(out=qk[:], in_=qk_banks[h][:].rearrange("p t c -> p (t c)"))
+            nc.vector.tensor_copy(out=qk[:], in_=qk_banks[h][:].rearrange("p t c -> p (t c)"))
             qk_t[h] = qk
 
         def tile_place(n):
@@ -354,12 +355,14 @@ def tile_refphi4flashdiffattention_pa_t_kernel(
                 accum_out=mean_sqs[j][:, ii : ii + 1],
             )
 
-        def finish(j):
+        def norm_factor(j):
             if not 0 <= j < N_HALF:
                 return
-            b, pr, g = j // 4, (j // 2) % PAIRS, j % 2
-            on_gpsimd = j < N_HALF - TAIL
-            if on_gpsimd:
+            var_eps = stats.tile([P, 2], F32, name="var_eps")
+            nc.gpsimd.tensor_scalar(
+                out=var_eps[:], in0=mean_sqs[j][:], scalar1=1.0, scalar2=EPS, op0=ALU.mult, op1=ALU.add
+            )
+            if j < N_HALF - TAIL:
                 xg = work.tile([P, 2, 2 * D], F32, name="xg")
                 nc.gpsimd.tensor_tensor(
                     out=xg[:],
@@ -367,18 +370,22 @@ def tile_refphi4flashdiffattention_pa_t_kernel(
                     in1=gain[:].unsqueeze(1).to_broadcast([P, 2, 2 * D]),
                     op=ALU.mult,
                 )
-            var_eps = stats.tile([P, 2], F32, name="var_eps")
-            nc.gpsimd.tensor_scalar(
-                out=var_eps[:], in0=mean_sqs[j][:], scalar1=1.0, scalar2=EPS, op0=ALU.mult, op1=ALU.add
-            )
+                gained[j] = xg
             rstd = stats.tile([P, 2], F32, name="rstd")
             nc.gpsimd.tensor_tensor(out=rstd[:], in0=var_eps[:], in1=neg_half[:], op=ALU.pow)
+            rstds[j] = rstd
+
+        def scale_and_store(j):
+            if not 0 <= j < N_HALF:
+                return
+            b, pr, g = j // 4, (j // 2) % PAIRS, j % 2
+            rstd = rstds[j]
             y = work.tile([P, 2, 2 * D], F32, name="y")
             for ii in range(2):
-                if on_gpsimd:
+                if j < N_HALF - TAIL:
                     nc.gpsimd.tensor_scalar(
                         out=y[:, ii, :],
-                        in0=xg[:, ii, :],
+                        in0=gained[j][:, ii, :],
                         scalar1=rstd[:, ii : ii + 1],
                         scalar2=0.0,
                         op0=ALU.mult,
@@ -406,7 +413,7 @@ def tile_refphi4flashdiffattention_pa_t_kernel(
         load_qk(1)
         load_v(1)
         lam_dots_and_gain()
-        for r in range(-3, N_HALF + 8):
+        for r in range(-3, N_HALF + 9):
             first = 4 * r
             if r >= 0 and r % 4 == 0 and r // 4 + 2 < B:
                 load_qk(r // 4 + 2)
@@ -449,4 +456,5 @@ def tile_refphi4flashdiffattention_pa_t_kernel(
             copy_e_words(r - 2, 0)
             difference(r - 5, 0)
             difference(r - 5, 1)
-            finish(r - 7)
+            norm_factor(r - 7)
+            scale_and_store(r - 8)

@@ -28,6 +28,7 @@ N_HEADS = B * H
 N_UNITS = B * PAIRS
 N_HALF = 2 * N_UNITS
 N_TILES = 4 * N_HALF
+TILES_OF = ((0, 3), (1, 2))
 E_SLOTS = 2
 TAIL = 4
 
@@ -192,7 +193,7 @@ def tile_refphi4flashdiffattention_pa_t_kernel(
 
         def tile_place(n):
             j, tau = divmod(n, 4)
-            return j, tau // 2, 2 * (j % 2) + tau % 2
+            return j, tau // 2, TILES_OF[j % 2][tau % 2]
 
         def score_matmuls(n):
             if not 0 <= n < N_TILES:
@@ -249,7 +250,7 @@ def tile_refphi4flashdiffattention_pa_t_kernel(
                 return
             et_ps = psum_et.tile([P, 2, 2, P], F32, name="et_ps")
             for ii in range(2):
-                e_words = e_tiles[((j // 2) % E_SLOTS, hh, 2 * (j % 2) + ii)][:].bitcast(F32)
+                e_words = e_tiles[((j // 2) % E_SLOTS, hh, TILES_OF[j % 2][ii])][:].bitcast(F32)
                 for u in range(2):
                     nc.tensor.transpose(
                         et_ps[:, ii, u, :], e_words[:, u * P : (u + 1) * P], ident_f32[:]
@@ -316,7 +317,7 @@ def tile_refphi4flashdiffattention_pa_t_kernel(
         def scale_second(j, ii):
             if not 0 <= j < N_HALF:
                 return
-            i = 2 * (j % 2) + ii
+            i = TILES_OF[j % 2][ii]
             second = work.tile([P, 2 * D], F32, name="second")
             nc.scalar.activation(
                 out=second[:],
@@ -329,7 +330,7 @@ def tile_refphi4flashdiffattention_pa_t_kernel(
         def difference(j, ii):
             if not 0 <= j < N_HALF:
                 return
-            i = 2 * (j % 2) + ii
+            i = TILES_OF[j % 2][ii]
             if ii == 0:
                 xs[j] = work.tile([P, 2, 2 * D], F32, name="x", bufs=5)
             nc.vector.scalar_tensor_tensor(
@@ -401,9 +402,9 @@ def tile_refphi4flashdiffattention_pa_t_kernel(
                         op1=ALU.mult,
                     )
             nc.sync.dma_start(
-                out=out[b, g * 2 * P : (g + 1) * 2 * P, 2 * pr : 2 * pr + 2, :].rearrange(
-                    "(i p) h d -> p i (h d)", p=P
-                ),
+                out=out[b, :, 2 * pr : 2 * pr + 2, :].rearrange("(i p) h d -> p i (h d)", p=P)[
+                    :, g : 4 - g : 3 - 2 * g, :
+                ],
                 in_=y[:],
             )
 

@@ -105,6 +105,7 @@ def tile_refphi4flashdiffattention_pa_t_kernel(
         xs = {}
         mean_sqs = {}
         gained = {}
+        variances = {}
         rstds = {}
 
         def load_qk(b):
@@ -150,27 +151,31 @@ def tile_refphi4flashdiffattention_pa_t_kernel(
                 op1=ALU.add,
             )
 
-        def regroup_v(b):
-            if not 0 <= b < B:
+        def regroup_v(h):
+            if not 0 <= h < N_HEADS:
                 return
-            grouped = work.tile([P, H * D, PACK], BF16, name="v_grouped", bufs=2, align_bytes=64)
+            head_cols = slice((h % H) * D, (h % H + 1) * D)
+            grouped = work.tile([P, D, PACK], BF16, name="v_grouped", bufs=2, align_bytes=64)
             nc.vector.tensor_copy(
                 out=grouped[:].rearrange("p (c i) t -> p c t i", i=4),
-                in_=v_inputs[b][:].rearrange("p t (c i) -> p c t i", i=4),
+                in_=v_inputs[h // H][:, :, head_cols].rearrange("p t (c i) -> p c t i", i=4),
             )
-            v_grouped[b] = grouped
+            v_grouped[h] = grouped
 
-        def quantise_v(b):
-            if not 0 <= b < B:
+        def quantise_v(h):
+            if not 0 <= h < N_HEADS:
                 return
-            v_codes = work.tile([P, H * D], U32, name="v_codes", bufs=3, align_bytes=64)
-            v_scales = work.tile([P, H * D], U8, name="v_scales", bufs=3, align_bytes=64)
+            if h % H == 0:
+                v_codes = work.tile([P, H * D], U32, name="v_codes", bufs=3, align_bytes=64)
+                v_scales = work.tile([P, H * D], U8, name="v_scales", bufs=3, align_bytes=64)
+                v_mx[h // H] = (v_codes, v_scales)
+            v_codes, v_scales = v_mx[h // H]
+            head_cols = slice((h % H) * D, (h % H + 1) * D)
             nc.vector.quantize_mx(
-                out=v_codes[:].bitcast(FP8X4),
-                scales=v_scales[:],
-                in_=v_grouped[b][:].rearrange("p f t -> p (f t)"),
+                out=v_codes[:, head_cols].bitcast(FP8X4),
+                scales=v_scales[:, head_cols],
+                in_=v_grouped[h][:].rearrange("p f t -> p (f t)"),
             )
-            v_mx[b] = (v_codes, v_scales)
 
         def transpose_qk(h):
             if not 0 <= h < N_HEADS:
@@ -356,24 +361,32 @@ def tile_refphi4flashdiffattention_pa_t_kernel(
                 accum_out=mean_sqs[j][:, ii : ii + 1],
             )
 
-        def norm_factor(j):
+        def times_gain(j):
+            if not 0 <= j < N_HALF - TAIL:
+                return
+            xg = work.tile([P, 2, 2 * D], F32, name="xg")
+            nc.gpsimd.tensor_tensor(
+                out=xg[:],
+                in0=xs[j][:],
+                in1=gain[:].unsqueeze(1).to_broadcast([P, 2, 2 * D]),
+                op=ALU.mult,
+            )
+            gained[j] = xg
+
+        def variance(j):
             if not 0 <= j < N_HALF:
                 return
             var_eps = stats.tile([P, 2], F32, name="var_eps")
             nc.gpsimd.tensor_scalar(
                 out=var_eps[:], in0=mean_sqs[j][:], scalar1=1.0, scalar2=EPS, op0=ALU.mult, op1=ALU.add
             )
-            if j < N_HALF - TAIL:
-                xg = work.tile([P, 2, 2 * D], F32, name="xg")
-                nc.gpsimd.tensor_tensor(
-                    out=xg[:],
-                    in0=xs[j][:],
-                    in1=gain[:].unsqueeze(1).to_broadcast([P, 2, 2 * D]),
-                    op=ALU.mult,
-                )
-                gained[j] = xg
+            variances[j] = var_eps
+
+        def norm_factor(j):
+            if not 0 <= j < N_HALF:
+                return
             rstd = stats.tile([P, 2], F32, name="rstd")
-            nc.gpsimd.tensor_tensor(out=rstd[:], in0=var_eps[:], in1=neg_half[:], op=ALU.pow)
+            nc.gpsimd.tensor_tensor(out=rstd[:], in0=variances[j][:], in1=neg_half[:], op=ALU.pow)
             rstds[j] = rstd
 
         def scale_and_store(j):
@@ -414,48 +427,48 @@ def tile_refphi4flashdiffattention_pa_t_kernel(
         load_qk(1)
         load_v(1)
         lam_dots_and_gain()
-        for r in range(-3, N_HALF + 9):
+        for r in range(-3, N_HALF + 7):
             first = 4 * r
             if r >= 0 and r % 4 == 0 and r // 4 + 2 < B:
                 load_qk(r // 4 + 2)
                 load_v(r // 4 + 2)
             score_matmuls(first + 2)
-            mx_passes(r - 5)
+            mx_passes(r - 4)
             exponentials(first - 4)
             row_maximum(first)
             copy_qk(r + 2)
-            sum_squares(r - 7, 1)
+            sum_squares(r - 5, 0)
+            sum_squares(r - 5, 1)
             score_matmuls(first + 3)
             transpose_e(r - 2, 0)
             exponentials(first - 3)
             row_maximum(first + 1)
             copy_e_words(r - 3, 1)
-            quantise_e(r - 4)
-            if r % 2 == 1:
-                reciprocals((r - 3) // 2)
             if r == 0:
                 lam_exps()
             score_matmuls(first + 4)
             transpose_qk(r + 3)
             exponentials(first - 2)
             row_maximum(first + 2)
-            scale_second(r - 5, 0)
-            scale_second(r - 5, 1)
-            if r % 4 == 1:
-                regroup_v(r // 4)
-            if r % 4 == 2:
-                quantise_v(r // 4)
-            if r == 1:
-                lam_value()
-            if r % 2 == 1:
-                times_lam((r - 3) // 2)
+            scale_second(r - 4, 0)
+            scale_second(r - 4, 1)
             score_matmuls(first + 5)
             transpose_e(r - 2, 1)
             exponentials(first - 1)
             row_maximum(first + 3)
-            sum_squares(r - 6, 0)
             copy_e_words(r - 2, 0)
-            difference(r - 5, 0)
-            difference(r - 5, 1)
-            norm_factor(r - 7)
-            scale_and_store(r - 8)
+            if r == 1:
+                lam_value()
+            regroup_v(r)
+            quantise_v(r - 1)
+            if r % 2 == 1:
+                reciprocals((r - 3) // 2)
+            quantise_e(r - 3)
+            if r % 2 == 1:
+                times_lam((r - 3) // 2)
+            difference(r - 4, 0)
+            difference(r - 4, 1)
+            times_gain(r - 4)
+            variance(r - 5)
+            scale_and_store(r - 6)
+            norm_factor(r - 5)

@@ -282,26 +282,25 @@ def tile_refphi4flashdiffattention_pa_t_kernel(
             )
             e_mx[j] = (codes, scales)
 
-        def mx_passes(j):
+        def mx_passes(j, hh):
             if not 0 <= j < N_HALF:
                 return
             v_codes, v_scales = v_mx[j // 4]
             codes, scales = e_mx[j]
             pair_cols = slice(((j // 2) % PAIRS) * 2 * D, ((j // 2) % PAIRS + 1) * 2 * D)
+            o_ps = psum_o.tile([P, 2, 2 * D], F32, name="o_ps")
             for ii in range(2):
                 q_cols = slice(ii * P, (ii + 1) * P)
-                o_ps = psum_o.tile([P, 2, 2 * D], F32, name="o_ps")
-                for hh in range(2):
-                    nc.tensor.matmul_mx(
-                        out=o_ps[:, hh, :],
-                        lhsT=codes[:, hh, q_cols].bitcast(FP8X4),
-                        lhsT_scale=scales[:, hh, q_cols],
-                        rhs=v_codes[:, pair_cols].bitcast(FP8X4),
-                        rhs_scale=v_scales[:, pair_cols],
-                        start=True,
-                        stop=True,
-                    )
-                out_banks[(j, ii)] = o_ps
+                nc.tensor.matmul_mx(
+                    out=o_ps[:, ii, :],
+                    lhsT=codes[:, hh, q_cols].bitcast(FP8X4),
+                    lhsT_scale=scales[:, hh, q_cols],
+                    rhs=v_codes[:, pair_cols].bitcast(FP8X4),
+                    rhs_scale=v_scales[:, pair_cols],
+                    start=True,
+                    stop=True,
+                )
+            out_banks[(j, hh)] = o_ps
 
         def reciprocals(unit):
             if not 0 <= unit < N_UNITS:
@@ -326,7 +325,7 @@ def tile_refphi4flashdiffattention_pa_t_kernel(
             second = work.tile([P, 2 * D], F32, name="second")
             nc.scalar.activation(
                 out=second[:],
-                in_=out_banks[(j, ii)][:, 1, :],
+                in_=out_banks[(j, 1)][:, ii, :],
                 func=ACT.Copy,
                 scale=lam_invs[j // 2][:, i : i + 1],
             )
@@ -340,7 +339,7 @@ def tile_refphi4flashdiffattention_pa_t_kernel(
                 xs[j] = work.tile([P, 2, 2 * D], F32, name="x", bufs=5)
             nc.vector.scalar_tensor_tensor(
                 out=xs[j][:, ii, :],
-                in0=out_banks[(j, ii)][:, 0, :],
+                in0=out_banks[(j, 0)][:, ii, :],
                 scalar=invs[j // 2][:, i : i + 1],
                 in1=seconds[(j, ii)][:],
                 op0=ALU.mult,
@@ -433,7 +432,7 @@ def tile_refphi4flashdiffattention_pa_t_kernel(
                 load_qk(r // 4 + 2)
                 load_v(r // 4 + 2)
             score_matmuls(first + 2)
-            mx_passes(r - 4)
+            mx_passes(r - 4, 1)
             exponentials(first - 4)
             row_maximum(first)
             copy_qk(r + 2)
@@ -447,6 +446,7 @@ def tile_refphi4flashdiffattention_pa_t_kernel(
             if r == 0:
                 lam_exps()
             score_matmuls(first + 4)
+            mx_passes(r - 4, 0)
             transpose_qk(r + 3)
             exponentials(first - 2)
             row_maximum(first + 2)

@@ -67,7 +67,7 @@ def tile_refphi4flashdiffattention_pa_t_kernel(
         )
         mask_bf = const.tile([P, P], BF16, name="mask_bf")
         nc.vector.tensor_copy(out=mask_bf[:], in_=mask_f32[:])
-        neg_half = const.tile([P, 2], F32, name="neg_half")
+        neg_half = const.tile([P, QT], F32, name="neg_half")
         nc.vector.memset(neg_half[:], -0.5)
 
         e_tiles = {}
@@ -349,21 +349,22 @@ def tile_refphi4flashdiffattention_pa_t_kernel(
         def sum_squares(j, ii):
             if not 0 <= j < N_HALF:
                 return
-            if ii == 0:
-                mean_sqs[j] = stats.tile([P, 2], F32, name="mean_sq")
+            if ii == 0 and j % 2 == 0:
+                mean_sqs[j // 2] = stats.tile([P, QT], F32, name="mean_sq")
+            c = 2 * (j % 2) + ii
             squares = work.tile([P, 2 * D], F32, name="squares")
             nc.scalar.activation(
                 out=squares[:],
                 in_=xs[j][:, ii, :],
                 func=ACT.Square,
                 scale=1.0 / math.sqrt(2 * D),
-                accum_out=mean_sqs[j][:, ii : ii + 1],
+                accum_out=mean_sqs[j // 2][:, c : c + 1],
             )
 
         def times_gain(j):
             if not 0 <= j < N_HALF - TAIL:
                 return
-            xg = work.tile([P, 2, 2 * D], F32, name="xg")
+            xg = work.tile([P, 2, 2 * D], F32, name="xg", bufs=5)
             nc.gpsimd.tensor_tensor(
                 out=xg[:],
                 in0=xs[j][:],
@@ -372,27 +373,27 @@ def tile_refphi4flashdiffattention_pa_t_kernel(
             )
             gained[j] = xg
 
-        def variance(j):
-            if not 0 <= j < N_HALF:
+        def variance(unit):
+            if not 0 <= unit < N_UNITS:
                 return
-            var_eps = stats.tile([P, 2], F32, name="var_eps")
+            var_eps = stats.tile([P, QT], F32, name="var_eps")
             nc.gpsimd.tensor_scalar(
-                out=var_eps[:], in0=mean_sqs[j][:], scalar1=1.0, scalar2=EPS, op0=ALU.mult, op1=ALU.add
+                out=var_eps[:], in0=mean_sqs[unit][:], scalar1=1.0, scalar2=EPS, op0=ALU.mult, op1=ALU.add
             )
-            variances[j] = var_eps
+            variances[unit] = var_eps
 
-        def norm_factor(j):
-            if not 0 <= j < N_HALF:
+        def norm_factor(unit):
+            if not 0 <= unit < N_UNITS:
                 return
-            rstd = stats.tile([P, 2], F32, name="rstd")
-            nc.gpsimd.tensor_tensor(out=rstd[:], in0=variances[j][:], in1=neg_half[:], op=ALU.pow)
-            rstds[j] = rstd
+            rstd = stats.tile([P, QT], F32, name="rstd")
+            nc.gpsimd.tensor_tensor(out=rstd[:], in0=variances[unit][:], in1=neg_half[:], op=ALU.pow)
+            rstds[unit] = rstd
 
         def scale_and_store(j):
             if not 0 <= j < N_HALF:
                 return
             b, pr, g = j // 4, (j // 2) % PAIRS, j % 2
-            rstd = rstds[j]
+            rstd = rstds[j // 2][:, 2 * g : 2 * g + 2]
             y = work.tile([P, 2, 2 * D], F32, name="y")
             for ii in range(2):
                 if j < N_HALF - TAIL:
@@ -426,7 +427,7 @@ def tile_refphi4flashdiffattention_pa_t_kernel(
         load_qk(1)
         load_v(1)
         lam_dots_and_gain()
-        for r in range(-3, N_HALF + 7):
+        for r in range(-3, N_HALF + 8):
             first = 4 * r
             if r >= 0 and r % 4 == 0 and r // 4 + 2 < B:
                 load_qk(r // 4 + 2)
@@ -469,6 +470,8 @@ def tile_refphi4flashdiffattention_pa_t_kernel(
             difference(r - 4, 0)
             difference(r - 4, 1)
             times_gain(r - 4)
-            variance(r - 5)
-            scale_and_store(r - 6)
-            norm_factor(r - 5)
+            if r % 2 == 0:
+                variance((r - 6) // 2)
+            scale_and_store(r - 7)
+            if r % 2 == 0:
+                norm_factor((r - 6) // 2)

@@ -30,7 +30,6 @@ N_HALF = 2 * N_UNITS
 N_TILES = 4 * N_HALF
 TILES_OF = ((0, 3), (1, 2))
 E_SLOTS = 2
-TAIL = 4
 
 FLOPS = 2 * B * H * S * S * D + 2 * B * H * S * S * 2 * D
 
@@ -156,9 +155,13 @@ def tile_refphi4flashdiffattention_pa_t_kernel(
                 return
             head_cols = slice((h % H) * D, (h % H + 1) * D)
             grouped = work.tile([P, D, PACK], BF16, name="v_grouped", bufs=2, align_bytes=64)
-            nc.vector.tensor_copy(
-                out=grouped[:].rearrange("p (c i) t -> p c t i", i=4),
-                in_=v_inputs[h // H][:, :, head_cols].rearrange("p t (c i) -> p c t i", i=4),
+            nc.gpsimd.tensor_scalar(
+                out=grouped[:],
+                in0=v_inputs[h // H][:, :, head_cols].rearrange("p t f -> p f t"),
+                scalar1=1.0,
+                scalar2=0.0,
+                op0=ALU.mult,
+                op1=ALU.add,
             )
             v_grouped[h] = grouped
 
@@ -362,7 +365,7 @@ def tile_refphi4flashdiffattention_pa_t_kernel(
             )
 
         def times_gain(j):
-            if not 0 <= j < N_HALF - TAIL:
+            if not 0 <= j < N_HALF:
                 return
             xg = work.tile([P, 2, 2 * D], F32, name="xg", bufs=5)
             nc.gpsimd.tensor_tensor(
@@ -393,27 +396,16 @@ def tile_refphi4flashdiffattention_pa_t_kernel(
             if not 0 <= j < N_HALF:
                 return
             b, pr, g = j // 4, (j // 2) % PAIRS, j % 2
-            rstd = rstds[j // 2][:, 2 * g : 2 * g + 2]
             y = work.tile([P, 2, 2 * D], F32, name="y")
             for ii in range(2):
-                if j < N_HALF - TAIL:
-                    nc.gpsimd.tensor_scalar(
-                        out=y[:, ii, :],
-                        in0=gained[j][:, ii, :],
-                        scalar1=rstd[:, ii : ii + 1],
-                        scalar2=0.0,
-                        op0=ALU.mult,
-                        op1=ALU.add,
-                    )
-                else:
-                    nc.vector.scalar_tensor_tensor(
-                        out=y[:, ii, :],
-                        in0=xs[j][:, ii, :],
-                        scalar=rstd[:, ii : ii + 1],
-                        in1=gain[:],
-                        op0=ALU.mult,
-                        op1=ALU.mult,
-                    )
+                c = 2 * g + ii
+                nc.vector.tensor_scalar(
+                    out=y[:, ii, :],
+                    in0=gained[j][:, ii, :],
+                    scalar1=rstds[j // 2][:, c : c + 1],
+                    scalar2=None,
+                    op0=ALU.mult,
+                )
             nc.sync.dma_start(
                 out=out[b, :, 2 * pr : 2 * pr + 2, :].rearrange("(i p) h d -> p i (h d)", p=P)[
                     :, g : 4 - g : 3 - 2 * g, :
@@ -460,8 +452,8 @@ def tile_refphi4flashdiffattention_pa_t_kernel(
             copy_e_words(r - 2, 0)
             if r == 1:
                 lam_value()
-            regroup_v(r)
             quantise_v(r - 1)
+            scale_and_store(r - 7)
             if r % 2 == 1:
                 reciprocals((r - 3) // 2)
             quantise_e(r - 3)
@@ -472,6 +464,6 @@ def tile_refphi4flashdiffattention_pa_t_kernel(
             times_gain(r - 4)
             if r % 2 == 0:
                 variance((r - 6) // 2)
-            scale_and_store(r - 7)
+            regroup_v(r)
             if r % 2 == 0:
                 norm_factor((r - 6) // 2)

@@ -154,7 +154,7 @@ def tile_refphi4flashdiffattention_pa_t_kernel(
             if not 0 <= h < N_HEADS:
                 return
             head_cols = slice((h % H) * D, (h % H + 1) * D)
-            grouped = work.tile([P, D, PACK], BF16, name="v_grouped", bufs=2, align_bytes=64)
+            grouped = work.tile([P, D, PACK], BF16, name="v_grouped", bufs=3, align_bytes=64)
             nc.gpsimd.tensor_scalar(
                 out=grouped[:],
                 in0=v_inputs[h // H][:, :, head_cols].rearrange("p t f -> p f t"),
@@ -367,7 +367,7 @@ def tile_refphi4flashdiffattention_pa_t_kernel(
         def times_gain(j):
             if not 0 <= j < N_HALF:
                 return
-            xg = work.tile([P, 2, 2 * D], F32, name="xg", bufs=5)
+            xg = work.tile([P, 2, 2 * D], F32, name="xg", bufs=6)
             nc.gpsimd.tensor_tensor(
                 out=xg[:],
                 in0=xs[j][:],
@@ -419,7 +419,7 @@ def tile_refphi4flashdiffattention_pa_t_kernel(
         load_qk(1)
         load_v(1)
         lam_dots_and_gain()
-        for r in range(-3, N_HALF + 8):
+        for r in range(-3, N_HALF + 9):
             first = 4 * r
             if r >= 0 and r % 4 == 0 and r // 4 + 2 < B:
                 load_qk(r // 4 + 2)
@@ -452,8 +452,8 @@ def tile_refphi4flashdiffattention_pa_t_kernel(
             copy_e_words(r - 2, 0)
             if r == 1:
                 lam_value()
-            quantise_v(r - 1)
-            scale_and_store(r - 7)
+            quantise_v(r - 2)
+            scale_and_store(r - 8)
             if r % 2 == 1:
                 reciprocals((r - 3) // 2)
             quantise_e(r - 3)

@@ -75,7 +75,7 @@ def tile_refphi4flashdiffattention_pa_t_kernel(
                 for i in range(QT):
                     e_t = const.tile([P, S], BF16, name="e_%d_%d_%d" % (slot, hh, i))
                     if i < QT - 1:
-                        nc.vector.memset(e_t[:, (i + 1) * P :], 0.0)
+                        nc.gpsimd.memset(e_t[:, (i + 1) * P :], 0.0)
                     e_tiles[(slot, hh, i)] = e_t
 
         lam_in = const.tile([P, 4, D], BF16, name="lam_in")
@@ -107,11 +107,17 @@ def tile_refphi4flashdiffattention_pa_t_kernel(
         variances = {}
         rstds = {}
 
-        def load_qk(b):
+        def load_qk(b, parts=1):
             q_sb = loads.tile([P, QT, H * D], BF16, name="q_sb")
-            nc.sync.dma_start(out=q_sb[:], in_=q[b].rearrange("(t p) h d -> p t (h d)", p=P))
             k_sb = loads.tile([P, QT, H * D], BF16, name="k_sb")
-            nc.sync.dma_start(out=k_sb[:], in_=k[b].rearrange("(t p) h d -> p t (h d)", p=P))
+            width = H * D // parts
+            for part in range(parts):
+                cols = slice(part * width, (part + 1) * width)
+                for sb, hbm in ((q_sb, q), (k_sb, k)):
+                    nc.sync.dma_start(
+                        out=sb[:, :, cols],
+                        in_=hbm[b].rearrange("(t p) h d -> p t (h d)", p=P)[:, :, cols],
+                    )
             qk_inputs[b] = (q_sb, k_sb)
 
         def load_v(b):
@@ -154,7 +160,7 @@ def tile_refphi4flashdiffattention_pa_t_kernel(
             if not 0 <= h < N_HEADS:
                 return
             head_cols = slice((h % H) * D, (h % H + 1) * D)
-            grouped = work.tile([P, D, PACK], BF16, name="v_grouped", bufs=3, align_bytes=64)
+            grouped = work.tile([P, D, PACK], BF16, name="v_grouped", bufs=2, align_bytes=64)
             nc.gpsimd.tensor_scalar(
                 out=grouped[:],
                 in0=v_inputs[h // H][:, :, head_cols].rearrange("p t f -> p f t"),
@@ -271,7 +277,8 @@ def tile_refphi4flashdiffattention_pa_t_kernel(
             if hh == 0:
                 e_grouped[j] = work.tile([P, 2, 2 * P * PACK], BF16, name="e_grouped", align_bytes=64)
             dst = e_grouped[j][:, hh, :].bitcast(F32).rearrange("p (i q u) -> p i q u", i=2, u=2)
-            nc.scalar.copy(out=dst, in_=word_banks[(j, hh)][:].rearrange("p i u q -> p i q u"))
+            copy = nc.vector.tensor_copy if j % 2 == 0 and hh == 1 else nc.scalar.copy
+            copy(out=dst, in_=word_banks[(j, hh)][:].rearrange("p i u q -> p i q u"))
 
         def quantise_e(j):
             if not 0 <= j < N_HALF:
@@ -413,12 +420,11 @@ def tile_refphi4flashdiffattention_pa_t_kernel(
                 in_=y[:],
             )
 
-        load_qk(0)
-        load_small()
+        load_qk(0, parts=PAIRS)
         load_v(0)
+        load_small()
         load_qk(1)
         load_v(1)
-        lam_dots_and_gain()
         for r in range(-3, N_HALF + 9):
             first = 4 * r
             if r >= 0 and r % 4 == 0 and r // 4 + 2 < B:
@@ -436,7 +442,7 @@ def tile_refphi4flashdiffattention_pa_t_kernel(
             exponentials(first - 3)
             row_maximum(first + 1)
             copy_e_words(r - 3, 1)
-            if r == 0:
+            if r == 1:
                 lam_exps()
             score_matmuls(first + 4)
             mx_passes(r - 4, 0)
@@ -450,20 +456,22 @@ def tile_refphi4flashdiffattention_pa_t_kernel(
             exponentials(first - 1)
             row_maximum(first + 3)
             copy_e_words(r - 2, 0)
-            if r == 1:
+            if r == 0:
+                lam_dots_and_gain()
+            if r == 2:
                 lam_value()
-            quantise_v(r - 2)
             scale_and_store(r - 8)
             if r % 2 == 1:
                 reciprocals((r - 3) // 2)
             quantise_e(r - 3)
             if r % 2 == 1:
                 times_lam((r - 3) // 2)
+            quantise_v(r - 2)
             difference(r - 4, 0)
             difference(r - 4, 1)
-            times_gain(r - 4)
+            regroup_v(r)
             if r % 2 == 0:
                 variance((r - 6) // 2)
-            regroup_v(r)
+            times_gain(r - 4)
             if r % 2 == 0:
                 norm_factor((r - 6) // 2)

@@ -29,6 +29,7 @@ N_UNITS = B * PAIRS
 N_HALF = 2 * N_UNITS
 N_TILES = 4 * N_HALF
 TILES_OF = ((0, 3), (1, 2))
+TAIL = 4
 E_SLOTS = 2
 
 FLOPS = 2 * B * H * S * S * D + 2 * B * H * S * S * 2 * D
@@ -202,7 +203,8 @@ def tile_refphi4flashdiffattention_pa_t_kernel(
             if not 0 <= h < N_HEADS:
                 return
             qk = work.tile([P, 2 * S], BF16, name="qk", bufs=6)
-            nc.vector.tensor_copy(out=qk[:], in_=qk_banks[h][:].rearrange("p t c -> p (t c)"))
+            copy = nc.scalar.copy if h == 1 else nc.vector.tensor_copy
+            copy(out=qk[:], in_=qk_banks[h][:].rearrange("p t c -> p (t c)"))
             qk_t[h] = qk
 
         def tile_place(n):
@@ -277,8 +279,7 @@ def tile_refphi4flashdiffattention_pa_t_kernel(
             if hh == 0:
                 e_grouped[j] = work.tile([P, 2, 2 * P * PACK], BF16, name="e_grouped", align_bytes=64)
             dst = e_grouped[j][:, hh, :].bitcast(F32).rearrange("p (i q u) -> p i q u", i=2, u=2)
-            copy = nc.vector.tensor_copy if j % 2 == 0 and hh == 1 else nc.scalar.copy
-            copy(out=dst, in_=word_banks[(j, hh)][:].rearrange("p i u q -> p i q u"))
+            nc.scalar.copy(out=dst, in_=word_banks[(j, hh)][:].rearrange("p i u q -> p i q u"))
 
         def quantise_e(j):
             if not 0 <= j < N_HALF:
@@ -323,8 +324,8 @@ def tile_refphi4flashdiffattention_pa_t_kernel(
             if not 0 <= unit < N_UNITS:
                 return
             lam_inv = stats.tile([P, QT], F32, name="lam_inv")
-            nc.vector.tensor_scalar(
-                out=lam_inv[:], in0=invs[unit][:, QT : 2 * QT], scalar1=lam[:], scalar2=None, op0=ALU.mult
+            nc.scalar.activation(
+                out=lam_inv[:], in_=invs[unit][:, QT : 2 * QT], func=ACT.Copy, scale=lam[:]
             )
             lam_invs[unit] = lam_inv
 
@@ -375,7 +376,8 @@ def tile_refphi4flashdiffattention_pa_t_kernel(
             if not 0 <= j < N_HALF:
                 return
             xg = work.tile([P, 2, 2 * D], F32, name="xg", bufs=6)
-            nc.gpsimd.tensor_tensor(
+            engine = nc.gpsimd if j < N_HALF - TAIL else nc.vector
+            engine.tensor_tensor(
                 out=xg[:],
                 in0=xs[j][:],
                 in1=gain[:].unsqueeze(1).to_broadcast([P, 2, 2 * D]),
@@ -442,6 +444,8 @@ def tile_refphi4flashdiffattention_pa_t_kernel(
             exponentials(first - 3)
             row_maximum(first + 1)
             copy_e_words(r - 3, 1)
+            if r % 2 == 0:
+                times_lam((r - 4) // 2)
             if r == 1:
                 lam_exps()
             score_matmuls(first + 4)
@@ -454,7 +458,6 @@ def tile_refphi4flashdiffattention_pa_t_kernel(
             score_matmuls(first + 5)
             transpose_e(r - 2, 1)
             exponentials(first - 1)
-            row_maximum(first + 3)
             copy_e_words(r - 2, 0)
             if r == 0:
                 lam_dots_and_gain()
@@ -464,11 +467,10 @@ def tile_refphi4flashdiffattention_pa_t_kernel(
             if r % 2 == 1:
                 reciprocals((r - 3) // 2)
             quantise_e(r - 3)
-            if r % 2 == 1:
-                times_lam((r - 3) // 2)
             quantise_v(r - 2)
             difference(r - 4, 0)
             difference(r - 4, 1)
+            row_maximum(first + 3)
             regroup_v(r)
             if r % 2 == 0:
                 variance((r - 6) // 2)

import math
from contextlib import ExitStack

import concourse.mybir as mybir
from concourse.masks import make_identity

BF16 = mybir.dt.bfloat16
F32 = mybir.dt.float32
U32 = mybir.dt.uint32
U8 = mybir.dt.uint8
FP8X4 = mybir.dt.float8_e4m3fn_x4
ALU = mybir.AluOpType
ACT = mybir.ActivationFunctionType
AXIS_X = mybir.AxisListType.X

B, S, H, D = 12, 512, 4, 128
P = 128
PAIRS = H // 2
QT = S // P
PACK = 4
DEPTH = 12
LAMBDA_INIT = 0.8 - 0.6 * math.exp(-0.3 * DEPTH)
NEG_INF = -1e30
EPS = 1e-5
SCALE = 1.0 / math.sqrt(D)

N_HEADS = B * H
N_UNITS = B * PAIRS
N_HALF = 2 * N_UNITS
N_TILES = 4 * N_HALF
TILES_OF = ((0, 3), (1, 2))
TAIL = 4
E_SLOTS = 2

FLOPS = 2 * B * H * S * S * D + 2 * B * H * S * S * 2 * D


def tile_refphi4flashdiffattention_pa_t_kernel(
    tc, q, k, v, lambda_q1, lambda_k1, lambda_q2, lambda_k2, subln_weight, out
):
    nc = tc.nc
    with ExitStack() as stack:
        const = stack.enter_context(tc.tile_pool(name="const", bufs=1))
        loads = stack.enter_context(tc.tile_pool(name="loads", bufs=3))
        work = stack.enter_context(tc.tile_pool(name="work", bufs=4))
        stats = stack.enter_context(tc.tile_pool(name="stats", bufs=4))
        psum_tp = stack.enter_context(tc.psum_pool(name="psum_tp", bufs=1))
        psum_s = stack.enter_context(tc.psum_pool(name="psum_s", bufs=3))
        psum_et = stack.enter_context(tc.psum_pool(name="psum_et", bufs=2))
        psum_o = stack.enter_context(tc.psum_pool(name="psum_o", bufs=2))
        stack.enter_context(tc.manual_schedule())

        ident_bf = const.tile([P, P], BF16, name="ident_bf")
        make_identity(nc, ident_bf[:])
        ident_f32 = const.tile([P, P], F32, name="ident_f32")
        make_identity(nc, ident_f32[:])
        mask_f32 = const.tile([P, P], F32, name="mask_f32")
        nc.gpsimd.memset(mask_f32[:], 0.0)
        nc.gpsimd.affine_select(
            out=mask_f32[:],
            in_=mask_f32[:],
            pattern=[[-1, P]],
            compare_op=ALU.is_ge,
            fill=NEG_INF,
            base=0,
            channel_multiplier=1,
        )
        mask_bf = const.tile([P, P], BF16, name="mask_bf")
        nc.vector.tensor_copy(out=mask_bf[:], in_=mask_f32[:])
        neg_half = const.tile([P, QT], F32, name="neg_half")
        nc.vector.memset(neg_half[:], -0.5)

        e_tiles = {}
        for slot in range(E_SLOTS):
            for hh in range(2):
                for i in range(QT):
                    e_t = const.tile([P, S], BF16, name="e_%d_%d_%d" % (slot, hh, i))
                    if i < QT - 1:
                        nc.gpsimd.memset(e_t[:, (i + 1) * P :], 0.0)
                    e_tiles[(slot, hh, i)] = e_t

        lam_in = const.tile([P, 4, D], BF16, name="lam_in")
        w_in = const.tile([P, 2 * D], BF16, name="w_in")
        dots = const.tile([P, 2], F32, name="dots")
        exps = const.tile([P, 2], F32, name="exps")
        lam = const.tile([P, 1], F32, name="lam")
        gain = const.tile([P, 2 * D], F32, name="gain")

        qk_inputs = {}
        v_inputs = {}
        v_grouped = {}
        v_mx = {}
        qk_banks = {}
        qk_t = {}
        score_banks = {}
        scores = {}
        rowsums = {}
        invs = {}
        lam_invs = {}
        word_banks = {}
        e_grouped = {}
        e_mx = {}
        out_banks = {}
        seconds = {}
        xs = {}
        mean_sqs = {}
        gained = {}
        variances = {}
        rstds = {}

        def load_qk(b, parts=1):
            q_sb = loads.tile([P, QT, H * D], BF16, name="q_sb")
            k_sb = loads.tile([P, QT, H * D], BF16, name="k_sb")
            width = H * D // parts
            for part in range(parts):
                cols = slice(part * width, (part + 1) * width)
                for sb, hbm in ((q_sb, q), (k_sb, k)):
                    nc.sync.dma_start(
                        out=sb[:, :, cols],
                        in_=hbm[b].rearrange("(t p) h d -> p t (h d)", p=P)[:, :, cols],
                    )
            qk_inputs[b] = (q_sb, k_sb)

        def load_v(b):
            v_sb = loads.tile([P, PACK, H * D], BF16, name="v_sb")
            nc.sync.dma_start(
                out=v_sb[:].rearrange("p (u e) f -> p u (e f)", u=2),
                in_=v[b].rearrange("(u p e) h d -> p u (e h d)", u=2, e=2),
            )
            v_inputs[b] = v_sb

        def load_small():
            for c, vec in enumerate((lambda_q1, lambda_q2, lambda_k1, lambda_k2)):
                nc.sync.dma_start(out=lam_in[:, c, :], in_=vec.partition_broadcast(P))
            nc.sync.dma_start(out=w_in[:], in_=subln_weight.partition_broadcast(P))

        def lam_dots_and_gain():
            prod = const.tile([P, 2, D], F32, name="prod")
            nc.vector.tensor_tensor(
                out=prod[:], in0=lam_in[:, 0:2, :], in1=lam_in[:, 2:4, :], op=ALU.mult
            )
            nc.vector.tensor_scalar(
                out=gain[:], in0=w_in[:], scalar1=1.0 - LAMBDA_INIT, scalar2=None, op0=ALU.mult
            )
            nc.vector.tensor_reduce(out=dots[:], in_=prod[:], axis=AXIS_X, op=ALU.add)

        def lam_exps():
            nc.scalar.activation(out=exps[:], in_=dots[:], func=ACT.Exp)

        def lam_value():
            nc.vector.tensor_scalar(
                out=lam[:],
                in0=exps[:, 0:1],
                scalar1=exps[:, 1:2],
                scalar2=LAMBDA_INIT,
                op0=ALU.subtract,
                op1=ALU.add,
            )

        def regroup_v(h):
            if not 0 <= h < N_HEADS:
                return
            head_cols = slice((h % H) * D, (h % H + 1) * D)
            grouped = work.tile([P, D, PACK], BF16, name="v_grouped", bufs=2, align_bytes=64)
            nc.gpsimd.tensor_scalar(
                out=grouped[:],
                in0=v_inputs[h // H][:, :, head_cols].rearrange("p t f -> p f t"),
                scalar1=1.0,
                scalar2=0.0,
                op0=ALU.mult,
                op1=ALU.add,
            )
            v_grouped[h] = grouped

        def quantise_v(h):
            if not 0 <= h < N_HEADS:
                return
            if h % H == 0:
                v_codes = work.tile([P, H * D], U32, name="v_codes", bufs=3, align_bytes=64)
                v_scales = work.tile([P, H * D], U8, name="v_scales", bufs=3, align_bytes=64)
                v_mx[h // H] = (v_codes, v_scales)
            v_codes, v_scales = v_mx[h // H]
            head_cols = slice((h % H) * D, (h % H + 1) * D)
            nc.vector.quantize_mx(
                out=v_codes[:, head_cols].bitcast(FP8X4),
                scales=v_scales[:, head_cols],
                in_=v_grouped[h][:].rearrange("p f t -> p (f t)"),
            )

        def transpose_qk(h):
            if not 0 <= h < N_HEADS:
                return
            q_sb, k_sb = qk_inputs[h // H]
            head_cols = slice((h % H) * D, (h % H + 1) * D)
            tp = psum_tp.tile([P, 2 * QT, P], BF16, name="tp")
            for t in range(QT):
                nc.tensor.transpose(tp[:, t, :], q_sb[:, t, head_cols], ident_bf[:])
            for t in range(QT):
                nc.tensor.transpose(tp[:, QT + t, :], k_sb[:, t, head_cols], ident_bf[:])
            qk_banks[h] = tp

        def copy_qk(h):
            if not 0 <= h < N_HEADS:
                return
            qk = work.tile([P, 2 * S], BF16, name="qk", bufs=6)
            copy = nc.scalar.copy if h == 1 else nc.vector.tensor_copy
            copy(out=qk[:], in_=qk_banks[h][:].rearrange("p t c -> p (t c)"))
            qk_t[h] = qk

        def tile_place(n):
            j, tau = divmod(n, 4)
            return j, tau // 2, TILES_OF[j % 2][tau % 2]

        def score_matmuls(n):
            if not 0 <= n < N_TILES:
                return
            j, hh, i = tile_place(n)
            q_t = qk_t[2 * (j // 2) + hh][:, 0:S]
            k_t = qk_t[2 * (j // 2) + hh][:, S : 2 * S]
            own = slice(i * P, (i + 1) * P)
            s_ps = psum_s.tile([P, S], F32, name="s_ps")
            nc.tensor.matmul(s_ps[:, own], lhsT=ident_bf[:], rhs=mask_bf[:], start=True, stop=False)
            nc.tensor.matmul(s_ps[:, own], lhsT=q_t[:, own], rhs=k_t[:, own], start=False, stop=True)
            if i > 0:
                nc.tensor.matmul(
                    s_ps[:, 0 : i * P], lhsT=q_t[:, own], rhs=k_t[:, 0 : i * P], start=True, stop=True
                )
            score_banks[n] = s_ps

        def row_maximum(n):
            if not 0 <= n < N_TILES:
                return
            width = (tile_place(n)[2] + 1) * P
            s_sb = work.tile([P, S], F32, name="s_sb", bufs=8)
            shift = stats.tile([P, 1], F32, name="shift", bufs=8)
            nc.vector.tensor_scalar(
                out=s_sb[:, 0:width],
                in0=score_banks[n][:, 0:width],
                scalar1=-SCALE,
                scalar2=None,
                op0=ALU.mult,
                op1=ALU.min,
                accum_out=shift[:],
            )
            scores[n] = (s_sb, shift)

        def exponentials(n):
            if not 0 <= n < N_TILES:
                return
            j, hh, i = tile_place(n)
            width = (i + 1) * P
            if n % 8 == 0:
                rowsums[j // 2] = stats.tile([P, 2 * QT], F32, name="rowsum")
            s_sb, shift = scores[n]
            nc.scalar.activation(
                out=e_tiles[((j // 2) % E_SLOTS, hh, i)][:, 0:width],
                in_=s_sb[:, 0:width],
                func=ACT.Exp,
                bias=shift[:],
                scale=-1.0,
                accum_out=rowsums[j // 2][:, QT * hh + i : QT * hh + i + 1],
            )

        def transpose_e(j, hh):
            if not 0 <= j < N_HALF:
                return
            et_ps = psum_et.tile([P, 2, 2, P], F32, name="et_ps")
            for ii in range(2):
                e_words = e_tiles[((j // 2) % E_SLOTS, hh, TILES_OF[j % 2][ii])][:].bitcast(F32)
                for u in range(2):
                    nc.tensor.transpose(
                        et_ps[:, ii, u, :], e_words[:, u * P : (u + 1) * P], ident_f32[:]
                    )
            word_banks[(j, hh)] = et_ps

        def copy_e_words(j, hh):
            if not 0 <= j < N_HALF:
                return
            if hh == 0:
                e_grouped[j] = work.tile([P, 2, 2 * P * PACK], BF16, name="e_grouped", align_bytes=64)
            dst = e_grouped[j][:, hh, :].bitcast(F32).rearrange("p (i q u) -> p i q u", i=2, u=2)
            nc.scalar.copy(out=dst, in_=word_banks[(j, hh)][:].rearrange("p i u q -> p i q u"))

        def quantise_e(j):
            if not 0 <= j < N_HALF:
                return
            codes = work.tile([P, 2, 2 * P], U32, name="codes", align_bytes=64)
            scales = work.tile([P, 2, 2 * P], U8, name="scales", align_bytes=64)
            nc.vector.quantize_mx(
                out=codes[:].rearrange("p h c -> p (h c)").bitcast(FP8X4),
                scales=scales[:].rearrange("p h c -> p (h c)"),
                in_=e_grouped[j][:].rearrange("p h c -> p (h c)"),
            )
            e_mx[j] = (codes, scales)

        def mx_passes(j, hh):
            if not 0 <= j < N_HALF:
                return
            v_codes, v_scales = v_mx[j // 4]
            codes, scales = e_mx[j]
            pair_cols = slice(((j // 2) % PAIRS) * 2 * D, ((j // 2) % PAIRS + 1) * 2 * D)
            o_ps = psum_o.tile([P, 2, 2 * D], F32, name="o_ps")
            for ii in range(2):
                q_cols = slice(ii * P, (ii + 1) * P)
                nc.tensor.matmul_mx(
                    out=o_ps[:, ii, :],
                    lhsT=codes[:, hh, q_cols].bitcast(FP8X4),
                    lhsT_scale=scales[:, hh, q_cols],
                    rhs=v_codes[:, pair_cols].bitcast(FP8X4),
                    rhs_scale=v_scales[:, pair_cols],
                    start=True,
                    stop=True,
                )
            out_banks[(j, hh)] = o_ps

        def reciprocals(unit):
            if not 0 <= unit < N_UNITS:
                return
            inv = stats.tile([P, 2 * QT], F32, name="inv")
            nc.vector.reciprocal(out=inv[:], in_=rowsums[unit][:])
            invs[unit] = inv

        def times_lam(unit):
            if not 0 <= unit < N_UNITS:
                return
            lam_inv = stats.tile([P, QT], F32, name="lam_inv")
            nc.scalar.activation(
                out=lam_inv[:], in_=invs[unit][:, QT : 2 * QT], func=ACT.Copy, scale=lam[:]
            )
            lam_invs[unit] = lam_inv

        def scale_second(j, ii):
            if not 0 <= j < N_HALF:
                return
            i = TILES_OF[j % 2][ii]
            second = work.tile([P, 2 * D], F32, name="second")
            nc.scalar.activation(
                out=second[:],
                in_=out_banks[(j, 1)][:, ii, :],
                func=ACT.Copy,
                scale=lam_invs[j // 2][:, i : i + 1],
            )
            seconds[(j, ii)] = second

        def difference(j, ii):
            if not 0 <= j < N_HALF:
                return
            i = TILES_OF[j % 2][ii]
            if ii == 0:
                xs[j] = work.tile([P, 2, 2 * D], F32, name="x", bufs=5)
            nc.vector.scalar_tensor_tensor(
                out=xs[j][:, ii, :],
                in0=out_banks[(j, 0)][:, ii, :],
                scalar=invs[j // 2][:, i : i + 1],
                in1=seconds[(j, ii)][:],
                op0=ALU.mult,
                op1=ALU.subtract,
            )

        def sum_squares(j, ii):
            if not 0 <= j < N_HALF:
                return
            if ii == 0 and j % 2 == 0:
                mean_sqs[j // 2] = stats.tile([P, QT], F32, name="mean_sq")
            c = 2 * (j % 2) + ii
            squares = work.tile([P, 2 * D], F32, name="squares")
            nc.scalar.activation(
                out=squares[:],
                in_=xs[j][:, ii, :],
                func=ACT.Square,
                scale=1.0 / math.sqrt(2 * D),
                accum_out=mean_sqs[j // 2][:, c : c + 1],
            )

        def times_gain(j):
            if not 0 <= j < N_HALF:
                return
            xg = work.tile([P, 2, 2 * D], F32, name="xg", bufs=6)
            engine = nc.gpsimd if j < N_HALF - TAIL else nc.vector
            engine.tensor_tensor(
                out=xg[:],
                in0=xs[j][:],
                in1=gain[:].unsqueeze(1).to_broadcast([P, 2, 2 * D]),
                op=ALU.mult,
            )
            gained[j] = xg

        def variance(unit):
            if not 0 <= unit < N_UNITS:
                return
            var_eps = stats.tile([P, QT], F32, name="var_eps")
            nc.gpsimd.tensor_scalar(
                out=var_eps[:], in0=mean_sqs[unit][:], scalar1=1.0, scalar2=EPS, op0=ALU.mult, op1=ALU.add
            )
            variances[unit] = var_eps

        def norm_factor(unit):
            if not 0 <= unit < N_UNITS:
                return
            rstd = stats.tile([P, QT], F32, name="rstd")
            nc.gpsimd.tensor_tensor(out=rstd[:], in0=variances[unit][:], in1=neg_half[:], op=ALU.pow)
            rstds[unit] = rstd

        def scale_and_store(j):
            if not 0 <= j < N_HALF:
                return
            b, pr, g = j // 4, (j // 2) % PAIRS, j % 2
            y = work.tile([P, 2, 2 * D], F32, name="y")
            for ii in range(2):
                c = 2 * g + ii
                nc.vector.tensor_scalar(
                    out=y[:, ii, :],
                    in0=gained[j][:, ii, :],
                    scalar1=rstds[j // 2][:, c : c + 1],
                    scalar2=None,
                    op0=ALU.mult,
                )
            nc.sync.dma_start(
                out=out[b, :, 2 * pr : 2 * pr + 2, :].rearrange("(i p) h d -> p i (h d)", p=P)[
                    :, g : 4 - g : 3 - 2 * g, :
                ],
                in_=y[:],
            )

        load_qk(0, parts=PAIRS)
        load_v(0)
        load_small()
        load_qk(1)
        load_v(1)
        for r in range(-3, N_HALF + 9):
            first = 4 * r
            if r >= 0 and r % 4 == 0 and r // 4 + 2 < B:
                load_qk(r // 4 + 2)
                load_v(r // 4 + 2)
            score_matmuls(first + 2)
            mx_passes(r - 4, 1)
            exponentials(first - 4)
            row_maximum(first)
            copy_qk(r + 2)
            sum_squares(r - 5, 0)
            sum_squares(r - 5, 1)
            score_matmuls(first + 3)
            transpose_e(r - 2, 0)
            exponentials(first - 3)
            row_maximum(first + 1)
            copy_e_words(r - 3, 1)
            if r % 2 == 0:
                times_lam((r - 4) // 2)
            if r == 1:
                lam_exps()
            score_matmuls(first + 4)
            mx_passes(r - 4, 0)
            transpose_qk(r + 3)
            exponentials(first - 2)
            row_maximum(first + 2)
            scale_second(r - 4, 0)
            scale_second(r - 4, 1)
            score_matmuls(first + 5)
            transpose_e(r - 2, 1)
            exponentials(first - 1)
            copy_e_words(r - 2, 0)
            if r == 0:
                lam_dots_and_gain()
            if r == 2:
                lam_value()
            scale_and_store(r - 8)
            if r % 2 == 1:
                reciprocals((r - 3) // 2)
            quantise_e(r - 3)
            quantise_v(r - 2)
            difference(r - 4, 0)
            difference(r - 4, 1)
            row_maximum(first + 3)
            regroup_v(r)
            if r % 2 == 0:
                variance((r - 6) // 2)
            times_gain(r - 4)
            if r % 2 == 0:
                norm_factor((r - 6) // 2)
